import numpy as np
import ml_dtypes


def mxq(x, axis, fmt="e4m3"):
    dtype, down = {"e4m3": (ml_dtypes.float8_e4m3fn, 7), "e5m2": (ml_dtypes.float8_e5m2, 14)}[fmt]
    v = np.moveaxis(np.asarray(x, np.float32).astype(ml_dtypes.bfloat16).astype(np.float64), axis, -1)
    blocks = v.reshape(v.shape[:-1] + (-1, 32))
    amax = np.abs(blocks).max(-1, keepdims=True)
    byte = np.maximum(np.where(amax > 0, np.frexp(amax)[1] - 1 + 127, 0) - down, 1)
    scale = np.exp2(byte - 127.0)
    codes = (blocks / scale).astype(np.float32).astype(dtype).astype(np.float64)
    return np.moveaxis((codes * scale).reshape(v.shape), -1, axis)


WIDE = False


def mx_kscale(k):
    if not WIDE:
        return np.ones(k)
    levels = np.array([10, -10, 5, -5, 0])
    a = np.random.permutation(np.resize(levels, k // 512 * 4)).reshape(k // 512, 4)
    idx = np.arange(k)
    return np.exp2(a[idx // 512, idx % 128 // 32])


BF16 = ml_dtypes.bfloat16


def bf(x):
    return np.asarray(x, np.float32).astype(BF16)


def f64(x):
    return np.asarray(x).astype(np.float64)


B, N, D, HID, HEADS = 4, 128, 3, 512, 128


def silu(v):
    e = np.exp(-np.abs(v))
    return v * np.where(v >= 0, 1.0, e) / (1.0 + e)


def pairwise_dist(c):
    diff = c[:, :, None, :] - c[:, None, :, :]
    sq = np.sum(diff * diff, axis=-1)
    safe = np.where(sq > 0, sq, 1.0)
    return np.where(sq > 0, np.sqrt(safe), 0.0)


def setup_inputs():
    t = np.maximum(mx_kscale(HID), 1.0) ** 2
    return {"coords": bf(np.random.standard_normal((B, N, D))),
            "w1": bf(np.random.uniform(-1.0, 1.0, (1, HID)) * t[None, :]),
            "b1": bf(np.random.uniform(-1.0, 1.0, HID) * t),
            "w2": bf(np.random.standard_normal((HID, HEADS)) / np.sqrt(HID) / t[:, None]),
            "b2": bf(np.random.standard_normal(HEADS) * 0.3)}


def reference(coords, w1, b1, w2, b2):
    d = pairwise_dist(f64(coords))
    h = silu(d[..., None] * f64(w1)[0] + f64(b1))
    b = (mxq(h, 3, "e4m3") @ mxq(f64(w2), 0, "e4m3")) + f64(b2)
    return np.transpose(b, (0, 3, 1, 2))

@@ -1,0 +1,238 @@
+from contextlib import ExitStack
+
+import concourse.mybir as mybir
+from concourse.masks import make_identity
+
+F32 = mybir.dt.float32
+BF16 = mybir.dt.bfloat16
+U32 = mybir.dt.uint32
+U8 = mybir.dt.uint8
+FP8X4 = mybir.dt.float8_e4m3fn_x4
+ACT = mybir.ActivationFunctionType
+ALU = mybir.AluOpType
+
+P = 128
+B = 4
+N = 128
+HID = 512
+HEADS = 128
+PACK = 4
+BANK = 512
+ROWS = 4
+GROUPS = N // ROWS
+HALF = GROUPS // 2
+
+FLOPS = 2 * B * N * N * HID * HEADS
+
+MIRROR_FROM_SBUF = True
+
+
+def on_scalar(g):
+    return g % 2 == 0
+
+
+def bank_plans():
+    def solo(b):
+        return ("solo", b, [(b, 0, 0)])
+
+    def pair(b, g):
+        return ("pair", (b, g), [(b, g, ROWS * g), (b, GROUPS - g, 0)])
+
+    def mid(k):
+        return ("mid", k, [(2 * k, HALF, N // 2), (2 * k + 1, HALF, 0)])
+
+    plans = [solo(0), solo(1)]
+    plans.extend([pair(0, g) for g in range(1, HALF)])
+    plans.append(mid(0))
+    plans.extend([pair(1, g) for g in range(1, HALF)])
+    plans.append(solo(2))
+    plans.extend([pair(2, g) for g in range(1, HALF)])
+    plans.append(mid(1))
+    plans.append(solo(3))
+    plans.extend([pair(3, g) for g in range(1, HALF)])
+    return plans
+
+
+def tile_distancerelativebias_kernel(tc, coords, w1, b1, w2, b2, out):
+    nc = tc.nc
+    with ExitStack() as ctx:
+        const = ctx.enter_context(tc.tile_pool(name="const", bufs=1))
+        hpool = ctx.enter_context(tc.tile_pool(name="hpool", bufs=3))
+        opool = ctx.enter_context(tc.tile_pool(name="opool", bufs=2))
+        vps = ctx.enter_context(tc.psum_pool(name="vps", bufs=1))
+        dps = ctx.enter_context(tc.psum_pool(name="dps", bufs=3))
+        ops = ctx.enter_context(tc.psum_pool(name="ops", bufs=4))
+
+        xj = const.tile([P, B, 3], BF16)
+        nc.sync.dma_start(out=xj[:], in_=coords.rearrange("b j c -> j b c"))
+        xbc = const.tile([P, B, N, 3], BF16)
+        nc.sync.dma_start(
+            out=xbc[:].rearrange("p b i c -> p (b i c)"),
+            in_=coords.rearrange("b i c -> (b i c)").partition_broadcast(P),
+        )
+        w1b = const.tile([P, PACK], BF16)
+        nc.sync.dma_start(out=w1b[:], in_=w1.rearrange("o (p t) -> (o p) t", t=PACK))
+        b1b = const.tile([P, PACK], BF16)
+        nc.sync.dma_start(out=b1b[:], in_=b1.rearrange("(p t) -> p t", t=PACK))
+        w2b = const.tile([P, PACK, HEADS], BF16)
+        nc.sync.dma_start(out=w2b[:], in_=w2.rearrange("(p t) m -> p t m", t=PACK))
+        b2b = const.tile([P, 1], BF16)
+        nc.sync.dma_start(out=b2b[:], in_=b2.rearrange("(p o) -> p o", o=1))
+
+        izz = const.tile([P, 3 * P], F32)
+        nc.gpsimd.memset(izz[:], 0.0)
+        make_identity(nc, izz[:, P:2 * P], nomemset=True)
+        ident = izz[:, P:2 * P]
+
+        one = const.tile([P, 1], F32)
+        nc.vector.memset(one[:], 1.0)
+        warm = const.tile([P, 1], F32)
+        nc.scalar.activation(out=warm[:], in_=one[:], func=ACT.Sqrt)
+
+        sq = const.tile([P, 3, B, N], F32)
+        for b in range(B):
+            for c in range(3):
+                nc.scalar.activation(
+                    out=sq[:, c, b, :], in_=xbc[:, b, :, c], func=ACT.Square,
+                    bias=xj[:, b, c:c + 1], scale=-1.0,
+                )
+        ssum = const.tile([P, B, N], F32)
+        nc.vector.tensor_tensor(out=ssum[:], in0=sq[:, 0], in1=sq[:, 1], op=ALU.add)
+        nc.vector.tensor_tensor(out=ssum[:], in0=ssum[:], in1=sq[:, 2], op=ALU.add)
+        dist = const.tile([P, B, N], F32)
+        nc.scalar.activation(out=dist[:], in_=ssum[:], func=ACT.Sqrt)
+
+        w1f = const.tile([P, PACK], F32)
+        nc.vector.tensor_copy(out=w1f[:], in_=w1b[:])
+        b1f = const.tile([P, PACK], F32)
+        nc.vector.tensor_copy(out=b1f[:], in_=b1b[:])
+        b2f = const.tile([P, 1], F32)
+        nc.vector.tensor_copy(out=b2f[:], in_=b2b[:])
+
+        dm = const.tile([P, B, N], F32)
+        nc.gpsimd.affine_select(
+            out=dm[:].rearrange("p b i -> p (b i)"), in_=dist[:].rearrange("p b i -> p (b i)"),
+            pattern=[[0, B], [-ROWS, GROUPS], [0, ROWS]], compare_op=ALU.is_ge, fill=0.0,
+            base=0, channel_multiplier=1,
+        )
+        vp = vps.tile([P, BANK], F32)
+        vpair = vp[:, 0:B * (N // 2)].rearrange("p (b i) -> p b i", b=B)
+        vmid = vp[:, B * (N // 2):B * (N // 2) + 2 * ROWS].rearrange("p (k r) -> p k r", k=2)
+        vs = const.tile([P, B, N // 2], F32)
+        vm = const.tile([P, 2, ROWS], F32)
+
+        def shifted(g_lo, g_hi):
+            for g in range(g_lo, g_hi):
+                w = 2 * P - ROWS * g
+                i2 = N - ROWS * g
+                nc.tensor.matmul(
+                    out=vpair[:, :, ROWS * g:ROWS * g + ROWS], lhsT=izz[:, w:w + P],
+                    rhs=dm[:, :, i2:i2 + ROWS], start=True, stop=True,
+                )
+            nc.vector.tensor_tensor(
+                out=vs[:, :, ROWS * g_lo:ROWS * g_hi], in0=dm[:, :, ROWS * g_lo:ROWS * g_hi],
+                in1=vpair[:, :, ROWS * g_lo:ROWS * g_hi], op=ALU.add,
+            )
+
+        shifted(1, 4)
+        shifted(4, HALF)
+        dmk = dm[:].rearrange("p (k e) i -> p k e i", e=2)
+        nc.tensor.matmul(
+            out=vmid, lhsT=izz[:, P + N // 2:2 * P + N // 2],
+            rhs=dmk[:, :, 1, N // 2:N // 2 + ROWS], start=True, stop=True,
+        )
+        nc.vector.tensor_tensor(out=vm[:], in0=dmk[:, :, 0, N // 2:N // 2 + ROWS], in1=vmid, op=ALU.add)
+
+        w2g = const.tile([P, HEADS, PACK], BF16, align_bytes=64)
+        nc.vector.tensor_copy(out=w2g[:], in_=w2b[:].rearrange("p t m -> p m t"))
+        w2c = const.tile([P, HEADS], U32, align_bytes=64)
+        w2s = const.tile([P, HEADS], U8, align_bytes=64)
+        nc.vector.quantize_mx(
+            out=w2c[:].bitcast(FP8X4), scales=w2s[:], in_=w2g[:].rearrange("p m t -> p (m t)")
+        )
+
+        otiles = {}
+        done = [set() for b in range(B)]
+        stored = [0 for b in range(B)]
+
+        for (kind, key, segments) in bank_plans():
+            dbank = dps.tile([P, BANK], F32, name="dbank")
+            for r in range(ROWS):
+                if kind == "solo":
+                    col = dist[:, key, r:r + 1]
+                elif kind == "pair":
+                    col = vs[:, key[0], ROWS * key[1] + r:ROWS * key[1] + r + 1]
+                else:
+                    col = vm[:, key, r:r + 1]
+                nc.tensor.transpose(dbank[:, r * P:(r + 1) * P], col.to_broadcast([P, P]), ident)
+            ht = hpool.tile([P, PACK, BANK], BF16, name="ht")
+            for t in range(PACK):
+                nc.scalar.activation(
+                    out=ht[:, t, :], in_=dbank[:], func=ACT.Silu,
+                    bias=b1f[:, t:t + 1], scale=w1f[:, t:t + 1],
+                )
+            grouped = hpool.tile([P, BANK, PACK], BF16, name="grouped", align_bytes=64)
+            nc.vector.tensor_copy(
+                out=grouped[:].rearrange("p (c i) t -> p c t i", i=4),
+                in_=ht[:].rearrange("p t (c i) -> p c t i", i=4),
+            )
+            codes = hpool.tile([P, BANK], U32, name="codes", align_bytes=64)
+            scales = hpool.tile([P, BANK], U8, name="scales", align_bytes=64)
+            nc.vector.quantize_mx(
+                out=codes[:].bitcast(FP8X4), scales=scales[:],
+                in_=grouped[:].rearrange("p w t -> p (w t)"),
+            )
+            obank = ops.tile([P, BANK], F32, name="obank")
+            nc.tensor.matmul_mx(
+                out=obank[:], lhsT=w2c[:].bitcast(FP8X4), lhsT_scale=w2s[:],
+                rhs=codes[:].bitcast(FP8X4), rhs_scale=scales[:], start=True, stop=True,
+            )
+            orn = obank[:].rearrange("p (r n) -> p r n", r=ROWS)
+            for (b, g, base) in segments:
+                if b not in otiles:
+                    otiles[b] = opool.tile([P, N * N], F32, name="ot")
+            for (b, g, base) in segments:
+                ov = otiles[b][:].rearrange("p (i j) -> p i j", j=N)
+                i0 = ROWS * g
+                length = N - i0
+                if on_scalar(g):
+                    nc.scalar.activation(
+                        out=ov[:, i0:i0 + ROWS, i0:N], in_=orn[:, :, base:base + length],
+                        func=ACT.Identity, bias=b2f[:, 0:1], scale=1.0,
+                    )
+                else:
+                    nc.vector.tensor_scalar(
+                        out=ov[:, i0:i0 + ROWS, i0:N], in0=orn[:, :, base:base + length],
+                        scalar1=b2f[:, 0:1], scalar2=None, op0=ALU.add,
+                    )
+            for (b, g, base) in segments:
+                ov = otiles[b][:].rearrange("p (i j) -> p i j", j=N)
+                i0 = ROWS * g
+                length = N - i0
+                if length > ROWS:
+                    if MIRROR_FROM_SBUF:
+                        nc.vector.tensor_copy(
+                            out=ov[:, i0 + ROWS:N, i0:i0 + ROWS],
+                            in_=ov[:, i0:i0 + ROWS, i0 + ROWS:N].rearrange("p r j -> p j r"),
+                        )
+                    else:
+                        nc.vector.tensor_scalar(
+                            out=ov[:, i0 + ROWS:N, i0:i0 + ROWS],
+                            in0=orn[:, :, base + ROWS:base + length].rearrange("p r n -> p n r"),
+                            scalar1=b2f[:, 0:1], scalar2=None, op0=ALU.add,
+                        )
+                done[b].add(g)
+            for b in sorted(set([s[0] for s in segments])):
+                complete = stored[b]
+                while complete < GROUPS and complete in done[b]:
+                    complete += 1
+                while complete - stored[b] >= 4:
+                    g0 = stored[b]
+                    lo = g0 * ROWS * N
+                    hi = (g0 + 4) * ROWS * N
+                    nc.sync.dma_start(
+                        out=out[b].rearrange("k i j -> k (i j)")[:, lo:hi],
+                        in_=otiles[b][:, lo:hi],
+                    )
+                    stored[b] = g0 + 4
+        assert stored == [GROUPS for b in range(B)]

@@ -21,47 +21,65 @@ BANK = 512
 ROWS = 4
 GROUPS = N // ROWS
 HALF = GROUPS // 2
+LAST = B - 1
+TAIL_SETS = [[17, 18], [19, 20], [21, 22, 23], [24, 25, 26, 27], [28, 29, 30, 31]]
+NBUF = 4
+AHEAD = 2
+LAG_GROUP = 2
+LAG_DIRECT = 3
+LAG_MIRROR = 4
 
 FLOPS = 2 * B * N * N * HID * HEADS
 
-MIRROR_FROM_SBUF = True
+PINNED = True
 
 
-def on_scalar(g):
-    return g % 2 == 0
+def on_scalar(b, g):
+    if b == LAST:
+        return g % 2 == 0
+    return g % 4 == 0
 
 
 def bank_plans():
-    def solo(b):
-        return ("solo", b, [(b, 0, 0)])
+    def solo(b, g):
+        return ("solo", (b, g), [(b, g, ROWS * g)], ROWS * g, N)
 
     def pair(b, g):
-        return ("pair", (b, g), [(b, g, ROWS * g), (b, GROUPS - g, 0)])
+        return ("pair", (b, g), [(b, g, ROWS * g), (b, GROUPS - g, 0)], 0, N)
 
     def mid(k):
-        return ("mid", k, [(2 * k, HALF, N // 2), (2 * k + 1, HALF, 0)])
+        return ("mid", k, [(2 * k, HALF, N // 2), (2 * k + 1, HALF, 0)], 0, N)
 
-    plans = [solo(0), solo(1)]
+    def tail(k):
+        segments = []
+        base = 0
+        for g in TAIL_SETS[k]:
+            segments.append((LAST, g, base))
+            base += N - ROWS * g
+        return ("tail", k, segments, 0, base)
+
+    plans = [solo(0, 0), solo(1, 0)]
     plans.extend([pair(0, g) for g in range(1, HALF)])
     plans.append(mid(0))
     plans.extend([pair(1, g) for g in range(1, HALF)])
-    plans.append(solo(2))
+    plans.append(solo(2, 0))
     plans.extend([pair(2, g) for g in range(1, HALF)])
     plans.append(mid(1))
-    plans.append(solo(3))
-    plans.extend([pair(3, g) for g in range(1, HALF)])
+    plans.extend([solo(LAST, g) for g in range(HALF)])
+    plans.extend([tail(k) for k in range(len(TAIL_SETS))])
     return plans
 
 
 def tile_distancerelativebias_kernel(tc, coords, w1, b1, w2, b2, out):
     nc = tc.nc
     with ExitStack() as ctx:
+        if PINNED:
+            ctx.enter_context(tc.manual_schedule())
         const = ctx.enter_context(tc.tile_pool(name="const", bufs=1))
-        hpool = ctx.enter_context(tc.tile_pool(name="hpool", bufs=3))
         opool = ctx.enter_context(tc.tile_pool(name="opool", bufs=2))
         vps = ctx.enter_context(tc.psum_pool(name="vps", bufs=1))
-        dps = ctx.enter_context(tc.psum_pool(name="dps", bufs=3))
-        ops = ctx.enter_context(tc.psum_pool(name="ops", bufs=4))
+        dps = ctx.enter_context(tc.psum_pool(name="dps", bufs=4))
+        ops = ctx.enter_context(tc.psum_pool(name="ops", bufs=3))
 
         xj = const.tile([P, B, 3], BF16)
         nc.sync.dma_start(out=xj[:], in_=coords.rearrange("b j c -> j b c"))
@@ -90,23 +108,29 @@ def tile_distancerelativebias_kernel(tc, coords, w1, b1, w2, b2, out):
         nc.scalar.activation(out=warm[:], in_=one[:], func=ACT.Sqrt)
 
         sq = const.tile([P, 3, B, N], F32)
-        for b in range(B):
+        ssum = const.tile([P, B, N], F32)
+        dist = const.tile([P, B, N], F32)
+        w1f = const.tile([P, PACK], F32)
+        b1f = const.tile([P, PACK], F32)
+        b2f = const.tile([P, 1], F32)
+
+        def squares(b):
             for c in range(3):
                 nc.scalar.activation(
                     out=sq[:, c, b, :], in_=xbc[:, b, :, c], func=ACT.Square,
                     bias=xj[:, b, c:c + 1], scale=-1.0,
                 )
-        ssum = const.tile([P, B, N], F32)
-        nc.vector.tensor_tensor(out=ssum[:], in0=sq[:, 0], in1=sq[:, 1], op=ALU.add)
-        nc.vector.tensor_tensor(out=ssum[:], in0=ssum[:], in1=sq[:, 2], op=ALU.add)
-        dist = const.tile([P, B, N], F32)
-        nc.scalar.activation(out=dist[:], in_=ssum[:], func=ACT.Sqrt)
+            nc.vector.tensor_tensor(out=ssum[:, b, :], in0=sq[:, 0, b, :], in1=sq[:, 1, b, :], op=ALU.add)
+            nc.vector.tensor_tensor(out=ssum[:, b, :], in0=ssum[:, b, :], in1=sq[:, 2, b, :], op=ALU.add)
 
-        w1f = const.tile([P, PACK], F32)
+        squares(0)
+        squares(1)
+        nc.scalar.activation(out=dist[:, 0, :], in_=ssum[:, 0, :], func=ACT.Sqrt)
         nc.vector.tensor_copy(out=w1f[:], in_=w1b[:])
-        b1f = const.tile([P, PACK], F32)
         nc.vector.tensor_copy(out=b1f[:], in_=b1b[:])
-        b2f = const.tile([P, 1], F32)
+        squares(2)
+        squares(3)
+        nc.scalar.activation(out=dist[:, 1:B, :], in_=ssum[:, 1:B, :], func=ACT.Sqrt)
         nc.vector.tensor_copy(out=b2f[:], in_=b2b[:])
 
         dm = const.tile([P, B, N], F32)
@@ -115,124 +139,210 @@ def tile_distancerelativebias_kernel(tc, coords, w1, b1, w2, b2, out):
             pattern=[[0, B], [-ROWS, GROUPS], [0, ROWS]], compare_op=ALU.is_ge, fill=0.0,
             base=0, channel_multiplier=1,
         )
+        dmk = dm[:].rearrange("p (k e) i -> p k e i", e=2)
+        n_tail = len(TAIL_SETS)
         vp = vps.tile([P, BANK], F32)
-        vpair = vp[:, 0:B * (N // 2)].rearrange("p (b i) -> p b i", b=B)
-        vmid = vp[:, B * (N // 2):B * (N // 2) + 2 * ROWS].rearrange("p (k r) -> p k r", k=2)
+        c_mid = B * (N // 2)
+        c_tail = c_mid + 2 * ROWS
+        vpair = vp[:, 0:c_mid].rearrange("p (b i) -> p b i", b=B)
+        vmid = vp[:, c_mid:c_tail].rearrange("p (k r) -> p k r", k=2)
+        vtail = vp[:, c_tail:c_tail + n_tail * ROWS].rearrange("p (k r) -> p k r", k=n_tail)
         vs = const.tile([P, B, N // 2], F32)
         vm = const.tile([P, 2, ROWS], F32)
-
-        def shifted(g_lo, g_hi):
-            for g in range(g_lo, g_hi):
-                w = 2 * P - ROWS * g
-                i2 = N - ROWS * g
-                nc.tensor.matmul(
-                    out=vpair[:, :, ROWS * g:ROWS * g + ROWS], lhsT=izz[:, w:w + P],
-                    rhs=dm[:, :, i2:i2 + ROWS], start=True, stop=True,
-                )
-            nc.vector.tensor_tensor(
-                out=vs[:, :, ROWS * g_lo:ROWS * g_hi], in0=dm[:, :, ROWS * g_lo:ROWS * g_hi],
-                in1=vpair[:, :, ROWS * g_lo:ROWS * g_hi], op=ALU.add,
-            )
-
-        shifted(1, 4)
-        shifted(4, HALF)
-        dmk = dm[:].rearrange("p (k e) i -> p k e i", e=2)
-        nc.tensor.matmul(
-            out=vmid, lhsT=izz[:, P + N // 2:2 * P + N // 2],
-            rhs=dmk[:, :, 1, N // 2:N // 2 + ROWS], start=True, stop=True,
-        )
-        nc.vector.tensor_tensor(out=vm[:], in0=dmk[:, :, 0, N // 2:N // 2 + ROWS], in1=vmid, op=ALU.add)
+        vt = const.tile([P, n_tail, ROWS], F32)
 
         w2g = const.tile([P, HEADS, PACK], BF16, align_bytes=64)
-        nc.vector.tensor_copy(out=w2g[:], in_=w2b[:].rearrange("p t m -> p m t"))
         w2c = const.tile([P, HEADS], U32, align_bytes=64)
         w2s = const.tile([P, HEADS], U8, align_bytes=64)
+        nc.vector.tensor_copy(out=w2g[:], in_=w2b[:].rearrange("p t m -> p m t"))
         nc.vector.quantize_mx(
             out=w2c[:].bitcast(FP8X4), scales=w2s[:], in_=w2g[:].rearrange("p m t -> p (m t)")
         )
 
+        hts = [const.tile([P, PACK, BANK], BF16, name="ht%d" % k) for k in range(NBUF)]
+        groupeds = [const.tile([P, BANK, PACK], BF16, name="grouped%d" % k, align_bytes=64) for k in range(NBUF)]
+        codess = [const.tile([P, BANK], U32, name="codes%d" % k, align_bytes=64) for k in range(NBUF)]
+        scaless = [const.tile([P, BANK], U8, name="scales%d" % k, align_bytes=64) for k in range(NBUF)]
+
+        plans = bank_plans()
+        n_banks = len(plans)
+        prepared = set()
+        dbanks = {}
+        obanks = {}
         otiles = {}
         done = [set() for b in range(B)]
         stored = [0 for b in range(B)]
 
-        for (kind, key, segments) in bank_plans():
-            dbank = dps.tile([P, BANK], F32, name="dbank")
+        def prep_key(s):
+            kind, key, segments, lo, hi = plans[s]
+            if kind == "pair":
+                return ("pair", key[1])
+            if kind == "solo":
+                return None
+            return (kind, key)
+
+        def prep_tensor(s):
+            pk = prep_key(s)
+            if pk is None or pk in prepared:
+                return None
+            prepared.add(pk)
+            kind, key = pk
+            if kind == "pair":
+                w = 2 * P - ROWS * key
+                i2 = N - ROWS * key
+                nc.tensor.matmul(
+                    out=vpair[:, :, ROWS * key:ROWS * key + ROWS], lhsT=izz[:, w:w + P],
+                    rhs=dm[:, :, i2:i2 + ROWS], start=True, stop=True,
+                )
+            elif kind == "mid":
+                nc.tensor.matmul(
+                    out=vmid[:, key, :], lhsT=izz[:, P + N // 2:2 * P + N // 2],
+                    rhs=dmk[:, key, 1, N // 2:N // 2 + ROWS], start=True, stop=True,
+                )
+            else:
+                segments = plans[s][2]
+                for q, (b, g, base) in enumerate(segments):
+                    w = P + ROWS * g - base
+                    nc.tensor.matmul(
+                        out=vtail[:, key, :], lhsT=izz[:, w:w + P],
+                        rhs=dm[:, b, ROWS * g:ROWS * g + ROWS],
+                        start=(q == 0), stop=(q == len(segments) - 1),
+                    )
+            return pk
+
+        def prep_vector(pk):
+            if pk is None:
+                return
+            kind, key = pk
+            if kind == "pair":
+                cols = slice(ROWS * key, ROWS * key + ROWS)
+                nc.vector.tensor_tensor(out=vs[:, :, cols], in0=dm[:, :, cols], in1=vpair[:, :, cols], op=ALU.add)
+            elif kind == "mid":
+                nc.vector.tensor_tensor(
+                    out=vm[:, key, :], in0=dmk[:, key, 0, N // 2:N // 2 + ROWS], in1=vmid[:, key, :], op=ALU.add
+                )
+            else:
+                nc.vector.tensor_copy(out=vt[:, key, :], in_=vtail[:, key, :])
+
+        def spread(s):
+            kind, key, segments, lo, hi = plans[s]
+            dbanks[s] = dps.tile([P, BANK], F32, name="dbank")
             for r in range(ROWS):
                 if kind == "solo":
-                    col = dist[:, key, r:r + 1]
+                    col = dist[:, key[0], ROWS * key[1] + r:ROWS * key[1] + r + 1]
                 elif kind == "pair":
                     col = vs[:, key[0], ROWS * key[1] + r:ROWS * key[1] + r + 1]
-                else:
+                elif kind == "mid":
                     col = vm[:, key, r:r + 1]
-                nc.tensor.transpose(dbank[:, r * P:(r + 1) * P], col.to_broadcast([P, P]), ident)
-            ht = hpool.tile([P, PACK, BANK], BF16, name="ht")
+                else:
+                    col = vt[:, key, r:r + 1]
+                nc.tensor.transpose(dbanks[s][:, r * P:(r + 1) * P], col.to_broadcast([P, P]), ident)
+
+        def hidden(s):
+            kind, key, segments, lo, hi = plans[s]
+            ht = hts[s % NBUF]
             for t in range(PACK):
                 nc.scalar.activation(
-                    out=ht[:, t, :], in_=dbank[:], func=ACT.Silu,
-                    bias=b1f[:, t:t + 1], scale=w1f[:, t:t + 1],
+                    out=ht[:, t, :].rearrange("p (r n) -> p r n", r=ROWS)[:, :, lo:hi],
+                    in_=dbanks[s][:].rearrange("p (r n) -> p r n", r=ROWS)[:, :, lo:hi],
+                    func=ACT.Silu, bias=b1f[:, t:t + 1], scale=w1f[:, t:t + 1],
                 )
-            grouped = hpool.tile([P, BANK, PACK], BF16, name="grouped", align_bytes=64)
-            nc.vector.tensor_copy(
-                out=grouped[:].rearrange("p (c i) t -> p c t i", i=4),
-                in_=ht[:].rearrange("p t (c i) -> p c t i", i=4),
-            )
-            codes = hpool.tile([P, BANK], U32, name="codes", align_bytes=64)
-            scales = hpool.tile([P, BANK], U8, name="scales", align_bytes=64)
+
+        def regroup(s):
+            kind, key, segments, lo, hi = plans[s]
+            ht = hts[s % NBUF]
+            grouped = groupeds[s % NBUF]
+            if lo == 0 and hi == N:
+                nc.vector.tensor_copy(
+                    out=grouped[:].rearrange("p (c i) t -> p c t i", i=4),
+                    in_=ht[:].rearrange("p t (c i) -> p c t i", i=4),
+                )
+            else:
+                nc.vector.tensor_copy(
+                    out=grouped[:].rearrange("p (r c i) t -> p r c t i", r=ROWS, i=4)[:, :, lo // 4:hi // 4],
+                    in_=ht[:].rearrange("p t (r c i) -> p r c t i", r=ROWS, i=4)[:, :, lo // 4:hi // 4],
+                )
+
+        def quantise(s):
             nc.vector.quantize_mx(
-                out=codes[:].bitcast(FP8X4), scales=scales[:],
-                in_=grouped[:].rearrange("p w t -> p (w t)"),
+                out=codess[s % NBUF][:].bitcast(FP8X4), scales=scaless[s % NBUF][:],
+                in_=groupeds[s % NBUF][:].rearrange("p w t -> p (w t)"),
             )
-            obank = ops.tile([P, BANK], F32, name="obank")
+
+        def multiply(s):
+            obanks[s] = ops.tile([P, BANK], F32, name="obank")
             nc.tensor.matmul_mx(
-                out=obank[:], lhsT=w2c[:].bitcast(FP8X4), lhsT_scale=w2s[:],
-                rhs=codes[:].bitcast(FP8X4), rhs_scale=scales[:], start=True, stop=True,
+                out=obanks[s][:], lhsT=w2c[:].bitcast(FP8X4), lhsT_scale=w2s[:],
+                rhs=codess[s % NBUF][:].bitcast(FP8X4), rhs_scale=scaless[s % NBUF][:],
+                start=True, stop=True,
             )
-            orn = obank[:].rearrange("p (r n) -> p r n", r=ROWS)
-            for (b, g, base) in segments:
+
+        def direct(s):
+            kind, key, segments, lo, hi = plans[s]
+            orn = obanks[s][:].rearrange("p (r n) -> p r n", r=ROWS)
+            ordered = [seg for seg in segments if not on_scalar(seg[0], seg[1])]
+            ordered.extend([seg for seg in segments if on_scalar(seg[0], seg[1])])
+            for (b, g, base) in ordered:
                 if b not in otiles:
                     otiles[b] = opool.tile([P, N * N], F32, name="ot")
-            for (b, g, base) in segments:
                 ov = otiles[b][:].rearrange("p (i j) -> p i j", j=N)
                 i0 = ROWS * g
-                length = N - i0
-                if on_scalar(g):
+                if on_scalar(b, g):
                     nc.scalar.activation(
-                        out=ov[:, i0:i0 + ROWS, i0:N], in_=orn[:, :, base:base + length],
+                        out=ov[:, i0:i0 + ROWS, i0:N], in_=orn[:, :, base:base + N - i0],
                         func=ACT.Identity, bias=b2f[:, 0:1], scale=1.0,
                     )
                 else:
                     nc.vector.tensor_scalar(
-                        out=ov[:, i0:i0 + ROWS, i0:N], in0=orn[:, :, base:base + length],
+                        out=ov[:, i0:i0 + ROWS, i0:N], in0=orn[:, :, base:base + N - i0],
                         scalar1=b2f[:, 0:1], scalar2=None, op0=ALU.add,
                     )
+
+        def mirror_and_store(s):
+            kind, key, segments, lo, hi = plans[s]
             for (b, g, base) in segments:
                 ov = otiles[b][:].rearrange("p (i j) -> p i j", j=N)
                 i0 = ROWS * g
-                length = N - i0
-                if length > ROWS:
-                    if MIRROR_FROM_SBUF:
-                        nc.vector.tensor_copy(
-                            out=ov[:, i0 + ROWS:N, i0:i0 + ROWS],
-                            in_=ov[:, i0:i0 + ROWS, i0 + ROWS:N].rearrange("p r j -> p j r"),
-                        )
-                    else:
-                        nc.vector.tensor_scalar(
-                            out=ov[:, i0 + ROWS:N, i0:i0 + ROWS],
-                            in0=orn[:, :, base + ROWS:base + length].rearrange("p r n -> p n r"),
-                            scalar1=b2f[:, 0:1], scalar2=None, op0=ALU.add,
-                        )
+                if i0 + ROWS < N:
+                    nc.vector.tensor_copy(
+                        out=ov[:, i0 + ROWS:N, i0:i0 + ROWS],
+                        in_=ov[:, i0:i0 + ROWS, i0 + ROWS:N].rearrange("p r j -> p j r"),
+                    )
                 done[b].add(g)
-            for b in sorted(set([s[0] for s in segments])):
+            for b in sorted(set([seg[0] for seg in segments])):
                 complete = stored[b]
                 while complete < GROUPS and complete in done[b]:
                     complete += 1
-                while complete - stored[b] >= 4:
+                chunk = 2 if (b == LAST and stored[b] >= HALF) else 4
+                while complete - stored[b] >= chunk:
                     g0 = stored[b]
-                    lo = g0 * ROWS * N
-                    hi = (g0 + 4) * ROWS * N
+                    g1 = min(complete, g0 + 4)
                     nc.sync.dma_start(
-                        out=out[b].rearrange("k i j -> k (i j)")[:, lo:hi],
-                        in_=otiles[b][:, lo:hi],
+                        out=out[b].rearrange("k i j -> k (i j)")[:, g0 * ROWS * N:g1 * ROWS * N],
+                        in_=otiles[b][:, g0 * ROWS * N:g1 * ROWS * N],
                     )
-                    stored[b] = g0 + 4
+                    stored[b] = g1
+
+        for s in range(AHEAD):
+            spread(s)
+        for s in range(AHEAD + 2):
+            prep_vector(prep_tensor(s))
+        for s in range(n_banks + LAG_MIRROR):
+            pk = None
+            if s + AHEAD < n_banks:
+                spread(s + AHEAD)
+            if s + AHEAD + 2 < n_banks:
+                pk = prep_tensor(s + AHEAD + 2)
+            if s < n_banks:
+                hidden(s)
+            if 0 <= s - LAG_GROUP < n_banks:
+                regroup(s - LAG_GROUP)
+            if 0 <= s - LAG_DIRECT < n_banks:
+                direct(s - LAG_DIRECT)
+            if 0 <= s - LAG_GROUP < n_banks:
+                quantise(s - LAG_GROUP)
+                multiply(s - LAG_GROUP)
+            if 0 <= s - LAG_MIRROR < n_banks:
+                mirror_and_store(s - LAG_MIRROR)
+            prep_vector(pk)
         assert stored == [GROUPS for b in range(B)]

@@ -35,9 +35,7 @@ PINNED = True
 
 
 def on_scalar(b, g):
-    if b == LAST:
-        return g % 2 == 0
-    return g % 4 == 0
+    return g % 2 == 0
 
 
 def bank_plans():

@@ -23,11 +23,12 @@ GROUPS = N // ROWS
 HALF = GROUPS // 2
 LAST = B - 1
 TAIL_SETS = [[17, 18], [19, 20], [21, 22, 23], [24, 25, 26, 27], [28, 29, 30, 31]]
-NBUF = 4
+UNIT = 2
+NUNIT = 3
+NQ = 2
 AHEAD = 2
-LAG_GROUP = 2
-LAG_DIRECT = 3
-LAG_MIRROR = 4
+LAG_DIRECT = 4
+LAG_MIRROR = 5
 
 FLOPS = 2 * B * N * N * HID * HEADS
 
@@ -35,7 +36,7 @@ PINNED = True
 
 
 def on_scalar(b, g):
-    return g % 2 == 0
+    return g % 2 == 0 and g % 8 != 2
 
 
 def bank_plans():
@@ -157,10 +158,10 @@ def tile_distancerelativebias_kernel(tc, coords, w1, b1, w2, b2, out):
             out=w2c[:].bitcast(FP8X4), scales=w2s[:], in_=w2g[:].rearrange("p m t -> p (m t)")
         )
 
-        hts = [const.tile([P, PACK, BANK], BF16, name="ht%d" % k) for k in range(NBUF)]
-        groupeds = [const.tile([P, BANK, PACK], BF16, name="grouped%d" % k, align_bytes=64) for k in range(NBUF)]
-        codess = [const.tile([P, BANK], U32, name="codes%d" % k, align_bytes=64) for k in range(NBUF)]
-        scaless = [const.tile([P, BANK], U8, name="scales%d" % k, align_bytes=64) for k in range(NBUF)]
+        hts = [const.tile([P, PACK, UNIT * BANK], BF16, name="ht%d" % k) for k in range(NUNIT)]
+        groupeds = [const.tile([P, UNIT * BANK, PACK], BF16, name="grouped%d" % k, align_bytes=64) for k in range(NQ)]
+        codess = [const.tile([P, UNIT * BANK], U32, name="codes%d" % k, align_bytes=64) for k in range(NQ)]
+        scaless = [const.tile([P, UNIT * BANK], U8, name="scales%d" % k, align_bytes=64) for k in range(NQ)]
 
         plans = bank_plans()
         n_banks = len(plans)
@@ -238,40 +239,63 @@ def tile_distancerelativebias_kernel(tc, coords, w1, b1, w2, b2, out):
 
         def hidden(s):
             kind, key, segments, lo, hi = plans[s]
-            ht = hts[s % NBUF]
+            u, half = place(s)
+            ht = hts[u % NUNIT]
             for t in range(PACK):
                 nc.scalar.activation(
-                    out=ht[:, t, :].rearrange("p (r n) -> p r n", r=ROWS)[:, :, lo:hi],
+                    out=ht[:, t, half:half + BANK].rearrange("p (r n) -> p r n", r=ROWS)[:, :, lo:hi],
                     in_=dbanks[s][:].rearrange("p (r n) -> p r n", r=ROWS)[:, :, lo:hi],
                     func=ACT.Silu, bias=b1f[:, t:t + 1], scale=w1f[:, t:t + 1],
                 )
 
-        def regroup(s):
-            kind, key, segments, lo, hi = plans[s]
-            ht = hts[s % NBUF]
-            grouped = groupeds[s % NBUF]
+        units = [[0], [1]]
+        units.extend([[q, q + 1] for q in range(2, n_banks - n_tail, UNIT)])
+        units.extend([[q] for q in range(n_banks - n_tail, n_banks)])
+        unit_of = {}
+        for u, plan_list in enumerate(units):
+            for q in plan_list:
+                unit_of[q] = u
+
+        def members(u):
+            return units[u]
+
+        def ends_unit(s):
+            return 0 <= s < n_banks and s == units[unit_of[s]][-1]
+
+        def place(s):
+            return unit_of[s], (s - units[unit_of[s]][0]) * BANK
+
+        def regroup(u):
+            lo = min([plans[q][3] for q in members(u)])
+            hi = max([plans[q][4] for q in members(u)])
+            width = len(members(u)) * BANK
+            ht = hts[u % NUNIT][:, :, 0:width]
+            grouped = groupeds[u % NQ][:, 0:width, :]
             if lo == 0 and hi == N:
                 nc.vector.tensor_copy(
-                    out=grouped[:].rearrange("p (c i) t -> p c t i", i=4),
-                    in_=ht[:].rearrange("p t (c i) -> p c t i", i=4),
+                    out=grouped.rearrange("p (c i) t -> p c t i", i=4),
+                    in_=ht.rearrange("p t (c i) -> p c t i", i=4),
                 )
             else:
                 nc.vector.tensor_copy(
-                    out=grouped[:].rearrange("p (r c i) t -> p r c t i", r=ROWS, i=4)[:, :, lo // 4:hi // 4],
-                    in_=ht[:].rearrange("p t (r c i) -> p r c t i", r=ROWS, i=4)[:, :, lo // 4:hi // 4],
+                    out=grouped.rearrange("p (r c i) t -> p r c t i", c=N // 4, i=4)[:, :, lo // 4:hi // 4],
+                    in_=ht.rearrange("p t (r c i) -> p r c t i", c=N // 4, i=4)[:, :, lo // 4:hi // 4],
                 )
 
-        def quantise(s):
+        def quantise(u):
+            width = len(members(u)) * BANK
             nc.vector.quantize_mx(
-                out=codess[s % NBUF][:].bitcast(FP8X4), scales=scaless[s % NBUF][:],
-                in_=groupeds[s % NBUF][:].rearrange("p w t -> p (w t)"),
+                out=codess[u % NQ][:, 0:width].bitcast(FP8X4), scales=scaless[u % NQ][:, 0:width],
+                in_=groupeds[u % NQ][:, 0:width, :].rearrange("p w t -> p (w t)"),
             )
 
         def multiply(s):
+            u, half = place(s)
             obanks[s] = ops.tile([P, BANK], F32, name="obank")
             nc.tensor.matmul_mx(
                 out=obanks[s][:], lhsT=w2c[:].bitcast(FP8X4), lhsT_scale=w2s[:],
-                rhs=codess[s % NBUF][:].bitcast(FP8X4), rhs_scale=scaless[s % NBUF][:],
+                rhs=codess[u % NQ][:, half:half + BANK].bitcast(FP8X4),
+                rhs_scale=scaless[u % NQ][:, half:half + BANK],
                 start=True, stop=True,
             )
 
@@ -333,13 +357,14 @@ def tile_distancerelativebias_kernel(tc, coords, w1, b1, w2, b2, out):
                 pk = prep_tensor(s + AHEAD + 2)
             if s < n_banks:
                 hidden(s)
-            if 0 <= s - LAG_GROUP < n_banks:
-                regroup(s - LAG_GROUP)
+            if ends_unit(s - 1):
+                regroup(unit_of[s - 1])
             if 0 <= s - LAG_DIRECT < n_banks:
                 direct(s - LAG_DIRECT)
-            if 0 <= s - LAG_GROUP < n_banks:
-                quantise(s - LAG_GROUP)
-                multiply(s - LAG_GROUP)
+            if ends_unit(s - 2):
+                quantise(unit_of[s - 2])
+                for q in members(unit_of[s - 2]):
+                    multiply(q)
             if 0 <= s - LAG_MIRROR < n_banks:
                 mirror_and_store(s - LAG_MIRROR)
             prep_vector(pk)

@@ -29,6 +29,7 @@ NQ = 2
 AHEAD = 2
 LAG_DIRECT = 4
 LAG_MIRROR = 5
+TAIL_PREP_AT = 18
 
 FLOPS = 2 * B * N * N * HID * HEADS
 
@@ -176,9 +177,9 @@ def tile_distancerelativebias_kernel(tc, coords, w1, b1, w2, b2, out):
             kind, key, segments, lo, hi = plans[s]
             if kind == "pair":
                 return ("pair", key[1])
-            if kind == "solo":
-                return None
-            return (kind, key)
+            if kind == "mid":
+                return ("mid", key)
+            return None
 
         def prep_tensor(s):
             pk = prep_key(s)
@@ -193,21 +194,22 @@ def tile_distancerelativebias_kernel(tc, coords, w1, b1, w2, b2, out):
                     out=vpair[:, :, ROWS * key:ROWS * key + ROWS], lhsT=izz[:, w:w + P],
                     rhs=dm[:, :, i2:i2 + ROWS], start=True, stop=True,
                 )
-            elif kind == "mid":
+            else:
                 nc.tensor.matmul(
                     out=vmid[:, key, :], lhsT=izz[:, P + N // 2:2 * P + N // 2],
                     rhs=dmk[:, key, 1, N // 2:N // 2 + ROWS], start=True, stop=True,
                 )
-            else:
-                segments = plans[s][2]
-                for q, (b, g, base) in enumerate(segments):
-                    w = P + ROWS * g - base
-                    nc.tensor.matmul(
-                        out=vtail[:, key, :], lhsT=izz[:, w:w + P],
-                        rhs=dm[:, b, ROWS * g:ROWS * g + ROWS],
-                        start=(q == 0), stop=(q == len(segments) - 1),
-                    )
             return pk
+
+        tail_shifts = [(k, q) for k in range(n_tail) for q in range(len(TAIL_SETS[k]))]
+
+        def shift_tail(k, q):
+            b, g, base = plans[n_banks - n_tail + k][2][q]
+            w = P + ROWS * g - base
+            nc.tensor.matmul(
+                out=vtail[:, k, :], lhsT=izz[:, w:w + P], rhs=dm[:, b, ROWS * g:ROWS * g + ROWS],
+                start=(q == 0), stop=(q == len(TAIL_SETS[k]) - 1),
+            )
 
         def prep_vector(pk):
             if pk is None:
@@ -216,12 +218,10 @@ def tile_distancerelativebias_kernel(tc, coords, w1, b1, w2, b2, out):
             if kind == "pair":
                 cols = slice(ROWS * key, ROWS * key + ROWS)
                 nc.vector.tensor_tensor(out=vs[:, :, cols], in0=dm[:, :, cols], in1=vpair[:, :, cols], op=ALU.add)
-            elif kind == "mid":
+            else:
                 nc.vector.tensor_tensor(
                     out=vm[:, key, :], in0=dmk[:, key, 0, N // 2:N // 2 + ROWS], in1=vmid[:, key, :], op=ALU.add
                 )
-            else:
-                nc.vector.tensor_copy(out=vt[:, key, :], in_=vtail[:, key, :])
 
         def spread(s):
             kind, key, segments, lo, hi = plans[s]
@@ -365,6 +365,10 @@ def tile_distancerelativebias_kernel(tc, coords, w1, b1, w2, b2, out):
                 quantise(unit_of[s - 2])
                 for q in members(unit_of[s - 2]):
                     multiply(q)
+            if 0 <= s - TAIL_PREP_AT < len(tail_shifts):
+                shift_tail(*tail_shifts[s - TAIL_PREP_AT])
+            if s - TAIL_PREP_AT == len(tail_shifts):
+                nc.vector.tensor_copy(out=vt[:], in_=vtail[:, :, :])
             if 0 <= s - LAG_MIRROR < n_banks:
                 mirror_and_store(s - LAG_MIRROR)
             prep_vector(pk)

@@ -28,7 +28,6 @@ NUNIT = 3
 NQ = 2
 AHEAD = 2
 LAG_DIRECT = 4
-LAG_MIRROR = 5
 TAIL_PREP_AT = 18
 
 FLOPS = 2 * B * N * N * HID * HEADS
@@ -37,6 +36,8 @@ PINNED = True
 
 
 def on_scalar(b, g):
+    if b == LAST and g > HALF:
+        return True
     return g % 2 == 0 and g % 8 != 2
 
 
@@ -262,6 +263,9 @@ def tile_distancerelativebias_kernel(tc, coords, w1, b1, w2, b2, out):
         def ends_unit(s):
             return 0 <= s < n_banks and s == units[unit_of[s]][-1]
 
+        def direct_step(q):
+            return q + LAG_DIRECT - (1 if len(units[unit_of[q]]) == 1 else 0)
+
         def place(s):
             return unit_of[s], (s - units[unit_of[s]][0]) * BANK
 
@@ -349,7 +353,7 @@ def tile_distancerelativebias_kernel(tc, coords, w1, b1, w2, b2, out):
             spread(s)
         for s in range(AHEAD + 2):
             prep_vector(prep_tensor(s))
-        for s in range(n_banks + LAG_MIRROR):
+        for s in range(n_banks + LAG_DIRECT + 1):
             pk = None
             if s + AHEAD < n_banks:
                 spread(s + AHEAD)
@@ -359,8 +363,9 @@ def tile_distancerelativebias_kernel(tc, coords, w1, b1, w2, b2, out):
                 hidden(s)
             if ends_unit(s - 1):
                 regroup(unit_of[s - 1])
-            if 0 <= s - LAG_DIRECT < n_banks:
-                direct(s - LAG_DIRECT)
+            for q in range(max(0, s - LAG_DIRECT), min(n_banks, s)):
+                if direct_step(q) == s:
+                    direct(q)
             if ends_unit(s - 2):
                 quantise(unit_of[s - 2])
                 for q in members(unit_of[s - 2]):
@@ -369,7 +374,8 @@ def tile_distancerelativebias_kernel(tc, coords, w1, b1, w2, b2, out):
                 shift_tail(*tail_shifts[s - TAIL_PREP_AT])
             if s - TAIL_PREP_AT == len(tail_shifts):
                 nc.vector.tensor_copy(out=vt[:], in_=vtail[:, :, :])
-            if 0 <= s - LAG_MIRROR < n_banks:
-                mirror_and_store(s - LAG_MIRROR)
+            for q in range(max(0, s - LAG_DIRECT - 1), min(n_banks, s)):
+                if direct_step(q) + 1 == s:
+                    mirror_and_store(q)
             prep_vector(pk)
         assert stored == [GROUPS for b in range(B)]

@@ -7,6 +7,7 @@ F32 = mybir.dt.float32
 BF16 = mybir.dt.bfloat16
 U32 = mybir.dt.uint32
 U8 = mybir.dt.uint8
+I32 = mybir.dt.int32
 FP8X4 = mybir.dt.float8_e4m3fn_x4
 ACT = mybir.ActivationFunctionType
 ALU = mybir.AluOpType
@@ -25,7 +26,11 @@ LAST = B - 1
 TAIL_SETS = [[17, 18], [19, 20], [21, 22, 23], [24, 25, 26, 27], [28, 29, 30, 31]]
 UNIT = 2
 NUNIT = 3
+NG = 3
 NQ = 2
+PARTS = 3
+PRODUCT_GROUPS = (6, 14)
+PRODUCT_LEAD = 5
 AHEAD = 2
 LAG_DIRECT = 4
 TAIL_PREP_AT = 18
@@ -38,7 +43,7 @@ PINNED = True
 def on_scalar(b, g):
     if b == LAST and g > HALF:
         return True
-    return g % 2 == 0 and g % 8 != 2
+    return g % 4 == 0
 
 
 def bank_plans():
@@ -85,10 +90,11 @@ def tile_distancerelativebias_kernel(tc, coords, w1, b1, w2, b2, out):
         xj = const.tile([P, B, 3], BF16)
         nc.sync.dma_start(out=xj[:], in_=coords.rearrange("b j c -> j b c"))
         xbc = const.tile([P, B, N, 3], BF16)
-        nc.sync.dma_start(
-            out=xbc[:].rearrange("p b i c -> p (b i c)"),
-            in_=coords.rearrange("b i c -> (b i c)").partition_broadcast(P),
-        )
+        for part in (slice(0, 1), slice(1, B)):
+            nc.sync.dma_start(
+                out=xbc[:, part].rearrange("p b i c -> p (b i c)"),
+                in_=coords[part].rearrange("b i c -> (b i c)").partition_broadcast(P),
+            )
         w1b = const.tile([P, PACK], BF16)
         nc.sync.dma_start(out=w1b[:], in_=w1.rearrange("o (p t) -> (o p) t", t=PACK))
         b1b = const.tile([P, PACK], BF16)
@@ -102,6 +108,14 @@ def tile_distancerelativebias_kernel(tc, coords, w1, b1, w2, b2, out):
         nc.gpsimd.memset(izz[:], 0.0)
         make_identity(nc, izz[:, P:2 * P], nomemset=True)
         ident = izz[:, P:2 * P]
+
+        mask = const.tile([P, B, N], F32)
+        nc.gpsimd.memset(mask[:], 1.0)
+        nc.gpsimd.affine_select(
+            out=mask[:].rearrange("p b i -> p (b i)"), in_=mask[:].rearrange("p b i -> p (b i)"),
+            pattern=[[0, B], [-ROWS, GROUPS], [0, ROWS]], compare_op=ALU.is_ge, fill=0.0,
+            base=0, channel_multiplier=1,
+        )
 
         one = const.tile([P, 1], F32)
         nc.vector.memset(one[:], 1.0)
@@ -121,33 +135,46 @@ def tile_distancerelativebias_kernel(tc, coords, w1, b1, w2, b2, out):
                     out=sq[:, c, b, :], in_=xbc[:, b, :, c], func=ACT.Square,
                     bias=xj[:, b, c:c + 1], scale=-1.0,
                 )
+
+        def add_first(b):
             nc.vector.tensor_tensor(out=ssum[:, b, :], in0=sq[:, 0, b, :], in1=sq[:, 1, b, :], op=ALU.add)
+
+        def add_last(b):
             nc.vector.tensor_tensor(out=ssum[:, b, :], in0=ssum[:, b, :], in1=sq[:, 2, b, :], op=ALU.add)
 
-        squares(0)
-        squares(1)
+        diff = const.tile([P, 3, N], F32)
+        xjf = const.tile([P, 3], F32)
+        nc.vector.tensor_copy(out=xjf[:], in_=xj[:, LAST, :])
+        for c in range(3):
+            nc.vector.tensor_scalar(
+                out=diff[:, c, :], in0=xbc[:, LAST, :, c], scalar1=xjf[:, c:c + 1], scalar2=None, op0=ALU.subtract,
+            )
+        for b in range(LAST):
+            squares(b)
+        add_first(0)
+        nc.vector.tensor_tensor(out=sq[:, :, LAST, :], in0=diff[:], in1=diff[:], op=ALU.mult)
+        add_last(0)
+        add_first(1)
+        add_first(LAST)
+        add_last(1)
+        add_last(LAST)
+        add_first(2)
+        add_last(2)
         nc.scalar.activation(out=dist[:, 0, :], in_=ssum[:, 0, :], func=ACT.Sqrt)
+        nc.scalar.activation(out=dist[:, 1:B, :], in_=ssum[:, 1:B, :], func=ACT.Sqrt)
         nc.vector.tensor_copy(out=w1f[:], in_=w1b[:])
         nc.vector.tensor_copy(out=b1f[:], in_=b1b[:])
-        squares(2)
-        squares(3)
-        nc.scalar.activation(out=dist[:, 1:B, :], in_=ssum[:, 1:B, :], func=ACT.Sqrt)
         nc.vector.tensor_copy(out=b2f[:], in_=b2b[:])
 
         dm = const.tile([P, B, N], F32)
-        nc.gpsimd.affine_select(
-            out=dm[:].rearrange("p b i -> p (b i)"), in_=dist[:].rearrange("p b i -> p (b i)"),
-            pattern=[[0, B], [-ROWS, GROUPS], [0, ROWS]], compare_op=ALU.is_ge, fill=0.0,
-            base=0, channel_multiplier=1,
-        )
+        nc.vector.tensor_tensor(out=dm[:], in0=dist[:], in1=mask[:], op=ALU.mult)
         dmk = dm[:].rearrange("p (k e) i -> p k e i", e=2)
         n_tail = len(TAIL_SETS)
         vp = vps.tile([P, BANK], F32)
         c_mid = B * (N // 2)
-        c_tail = c_mid + 2 * ROWS
         vpair = vp[:, 0:c_mid].rearrange("p (b i) -> p b i", b=B)
-        vmid = vp[:, c_mid:c_tail].rearrange("p (k r) -> p k r", k=2)
-        vtail = vp[:, c_tail:c_tail + n_tail * ROWS].rearrange("p (k r) -> p k r", k=n_tail)
+        vtail = vp[:, c_mid:c_mid + n_tail * ROWS].rearrange("p (k r) -> p k r", k=n_tail)
+        vrow = vp[:, c_mid:BANK].bitcast(BF16).rearrange("p (b j) -> p b j", b=B)
         vs = const.tile([P, B, N // 2], F32)
         vm = const.tile([P, 2, ROWS], F32)
         vt = const.tile([P, n_tail, ROWS], F32)
@@ -161,9 +188,27 @@ def tile_distancerelativebias_kernel(tc, coords, w1, b1, w2, b2, out):
         )
 
         hts = [const.tile([P, PACK, UNIT * BANK], BF16, name="ht%d" % k) for k in range(NUNIT)]
-        groupeds = [const.tile([P, UNIT * BANK, PACK], BF16, name="grouped%d" % k, align_bytes=64) for k in range(NQ)]
+        groupeds = [const.tile([P, UNIT * BANK, PACK], BF16, name="grouped%d" % k, align_bytes=64) for k in range(NG)]
         codess = [const.tile([P, UNIT * BANK], U32, name="codes%d" % k, align_bytes=64) for k in range(NQ)]
         scaless = [const.tile([P, UNIT * BANK], U8, name="scales%d" % k, align_bytes=64) for k in range(NQ)]
+
+        wsel = const.tile([P, ROWS, HID], BF16)
+        nc.gpsimd.memset(wsel[:].rearrange("p r c -> p (r c)").bitcast(I32), 0)
+        for r in range(ROWS):
+            nc.sync.dma_start(
+                out=wsel[PARTS * r:PARTS * (r + 1), r, :], in_=w1.rearrange("o c -> (o c)").partition_broadcast(PARTS)
+            )
+            nc.sync.dma_start(out=wsel[P - 1:P, r, :], in_=b1.rearrange("(o c) -> o c", o=1))
+        identb = const.tile([P, P], BF16)
+        nc.gpsimd.tensor_copy(out=identb[:], in_=ident)
+        parts = {}
+        drows = {}
+        for g in PRODUCT_GROUPS:
+            parts[g] = const.tile([P, B, P], BF16, name="parts%d" % g)
+            drows[g] = const.tile([P, B, P], BF16, name="drow%d" % g)
+            nc.gpsimd.memset(parts[g][:].rearrange("p b m -> p (b m)").bitcast(I32), 0)
+            nc.gpsimd.memset(parts[g][:, :, P - 1:P], 1.0)
+        rests = [const.tile([P, B, ROWS], F32, name="rest%d" % e) for e in range(PARTS - 1)]
 
         plans = bank_plans()
         n_banks = len(plans)
@@ -197,7 +242,7 @@ def tile_distancerelativebias_kernel(tc, coords, w1, b1, w2, b2, out):
                 )
             else:
                 nc.tensor.matmul(
-                    out=vmid[:, key, :], lhsT=izz[:, P + N // 2:2 * P + N // 2],
+                    out=vpair[:, key, 0:ROWS], lhsT=izz[:, P + N // 2:2 * P + N // 2],
                     rhs=dmk[:, key, 1, N // 2:N // 2 + ROWS], start=True, stop=True,
                 )
             return pk
@@ -221,8 +266,36 @@ def tile_distancerelativebias_kernel(tc, coords, w1, b1, w2, b2, out):
                 nc.vector.tensor_tensor(out=vs[:, :, cols], in0=dm[:, :, cols], in1=vpair[:, :, cols], op=ALU.add)
             else:
                 nc.vector.tensor_tensor(
-                    out=vm[:, key, :], in0=dmk[:, key, 0, N // 2:N // 2 + ROWS], in1=vmid[:, key, :], op=ALU.add
+                    out=vm[:, key, :], in0=dmk[:, key, 0, N // 2:N // 2 + ROWS], in1=vpair[:, key, 0:ROWS], op=ALU.add
                 )
+
+        def product_group(s):
+            kind, key = plans[s][0:2]
+            return key[1] if kind in ("pair", "solo") and key[1] in PRODUCT_GROUPS else None
+
+        def split(g):
+            rest = vs[:, :, ROWS * g:ROWS * g + ROWS]
+            pieces = parts[g][:, :, 0:PARTS * ROWS].rearrange("p b (r e) -> p b r e", e=PARTS)
+            for e in range(PARTS):
+                nc.gpsimd.tensor_copy(out=pieces[:, :, :, e], in_=rest)
+                if e + 1 < PARTS:
+                    nc.gpsimd.tensor_tensor(out=rests[e][:], in0=rest, in1=pieces[:, :, :, e], op=ALU.subtract)
+                    rest = rests[e][:]
+
+        def turn(g):
+            for b in range(B):
+                nc.tensor.transpose(vrow[:, b, :], parts[g][:, b, :], identb[:])
+
+        def product(s, rows):
+            kind, key, segments, lo, hi = plans[s]
+            for r in rows:
+                dbanks[s, r] = dps.tile([P, BANK], F32, name="dbank")
+                weights = wsel[:, r, :].rearrange("p (m t) -> p t m", t=PACK)
+                for t in range(PACK):
+                    nc.tensor.matmul(
+                        out=dbanks[s, r][:, t * N + lo:t * N + hi], lhsT=weights[:, t, :],
+                        rhs=drows[key[1]][:, key[0], lo:hi], start=True, stop=True,
+                    )
 
         def spread(s):
             kind, key, segments, lo, hi = plans[s]
@@ -241,6 +314,13 @@ def tile_distancerelativebias_kernel(tc, coords, w1, b1, w2, b2, out):
         def hidden(s):
             kind, key, segments, lo, hi = plans[s]
             u, half = place(s)
+            if product_group(s) is not None:
+                for r in range(ROWS):
+                    nc.scalar.activation(
+                        out=groupeds[u % NG][:, half + r * N + lo:half + r * N + hi, :],
+                        in_=dbanks[s, r][:].rearrange("p (t n) -> p n t", t=PACK)[:, lo:hi, :], func=ACT.Silu,
+                    )
+                return
             ht = hts[u % NUNIT]
             for t in range(PACK):
                 nc.scalar.activation(
@@ -270,11 +350,13 @@ def tile_distancerelativebias_kernel(tc, coords, w1, b1, w2, b2, out):
             return unit_of[s], (s - units[unit_of[s]][0]) * BANK
 
         def regroup(u):
-            lo = min([plans[q][3] for q in members(u)])
-            hi = max([plans[q][4] for q in members(u)])
-            width = len(members(u)) * BANK
-            ht = hts[u % NUNIT][:, :, 0:width]
-            grouped = groupeds[u % NQ][:, 0:width, :]
+            plain = [q for q in members(u) if product_group(q) is None]
+            lo = min([plans[q][3] for q in plain])
+            hi = max([plans[q][4] for q in plain])
+            first = place(plain[0])[1]
+            last = place(plain[-1])[1] + BANK
+            ht = hts[u % NUNIT][:, :, first:last]
+            grouped = groupeds[u % NG][:, first:last, :]
             if lo == 0 and hi == N:
                 nc.vector.tensor_copy(
                     out=grouped.rearrange("p (c i) t -> p c t i", i=4),
@@ -290,7 +372,7 @@ def tile_distancerelativebias_kernel(tc, coords, w1, b1, w2, b2, out):
             width = len(members(u)) * BANK
             nc.vector.quantize_mx(
                 out=codess[u % NQ][:, 0:width].bitcast(FP8X4), scales=scaless[u % NQ][:, 0:width],
-                in_=groupeds[u % NQ][:, 0:width, :].rearrange("p w t -> p (w t)"),
+                in_=groupeds[u % NG][:, 0:width, :].rearrange("p w t -> p (w t)"),
             )
 
         def multiply(s):
@@ -349,18 +431,40 @@ def tile_distancerelativebias_kernel(tc, coords, w1, b1, w2, b2, out):
                     )
                     stored[b] = g1
 
+        first_use = {}
+        for s in range(n_banks):
+            if product_group(s) is not None:
+                first_use.setdefault(product_group(s), s)
+        spread_at = {}
+        for s in range(AHEAD, n_banks):
+            if product_group(s) is None:
+                late = product_group(s - 1) is not None or product_group(s - 2) is not None
+                if not late:
+                    spread_at.setdefault(s - AHEAD, []).append(s)
+
         for s in range(AHEAD):
             spread(s)
         for s in range(AHEAD + 2):
             prep_vector(prep_tensor(s))
         for s in range(n_banks + LAG_DIRECT + 1):
-            pk = None
-            if s + AHEAD < n_banks:
-                spread(s + AHEAD)
+            pks = []
+            for lead, rows in ((1, (2,)), (2, (0, 1))):
+                if s + lead < n_banks and product_group(s + lead) is not None:
+                    product(s + lead, rows)
+            for q in spread_at.get(s, []):
+                spread(q)
             if s + AHEAD + 2 < n_banks:
-                pk = prep_tensor(s + AHEAD + 2)
+                pks.append(prep_tensor(s + AHEAD + 2))
+            for g in PRODUCT_GROUPS:
+                if s + PRODUCT_LEAD == first_use[g]:
+                    pks.append(prep_tensor(first_use[g]))
             if s < n_banks:
                 hidden(s)
+            if s + 1 < n_banks and product_group(s + 1) is not None:
+                product(s + 1, (3,))
+            if s < n_banks and product_group(s) is not None:
+                spread(s + 1)
+                spread(s + 2)
             if ends_unit(s - 1):
                 regroup(unit_of[s - 1])
             for q in range(max(0, s - LAG_DIRECT), min(n_banks, s)):
@@ -377,5 +481,15 @@ def tile_distancerelativebias_kernel(tc, coords, w1, b1, w2, b2, out):
             for q in range(max(0, s - LAG_DIRECT - 1), min(n_banks, s)):
                 if direct_step(q) + 1 == s:
                     mirror_and_store(q)
-            prep_vector(pk)
+            for pk in pks:
+                prep_vector(pk)
+            for g in PRODUCT_GROUPS:
+                if s + PRODUCT_LEAD == first_use[g]:
+                    split(g)
+                if s + PRODUCT_LEAD - 1 == first_use[g]:
+                    turn(g)
+                if s + PRODUCT_LEAD - 2 == first_use[g]:
+                    nc.vector.tensor_copy(
+                        out=drows[g][:].rearrange("p b j -> p (b j)"), in_=vrow.rearrange("p b j -> p (b j)")
+                    )
         assert stored == [GROUPS for b in range(B)]

@@ -41,8 +41,8 @@ PINNED = True
 
 
 def on_scalar(b, g):
-    if b == LAST and g > HALF:
-        return True
+    if b == LAST:
+        return g > HALF or g % 2 == 0
     return g % 4 == 0
 
 
@@ -87,10 +87,11 @@ def tile_distancerelativebias_kernel(tc, coords, w1, b1, w2, b2, out):
         dps = ctx.enter_context(tc.psum_pool(name="dps", bufs=4))
         ops = ctx.enter_context(tc.psum_pool(name="ops", bufs=3))
 
-        xj = const.tile([P, B, 3], BF16)
-        nc.sync.dma_start(out=xj[:], in_=coords.rearrange("b j c -> j b c"))
+        xj0 = const.tile([P, 1, 3], BF16)
+        xjr = const.tile([P, B - 1, 3], BF16)
         xbc = const.tile([P, B, N, 3], BF16)
-        for part in (slice(0, 1), slice(1, B)):
+        for part, xj in ((slice(0, 1), xj0), (slice(1, B), xjr)):
+            nc.scalar.dma_start(out=xj[:], in_=coords[part].rearrange("b j c -> j b c"))
             nc.sync.dma_start(
                 out=xbc[:, part].rearrange("p b i c -> p (b i c)"),
                 in_=coords[part].rearrange("b i c -> (b i c)").partition_broadcast(P),
@@ -133,7 +134,7 @@ def tile_distancerelativebias_kernel(tc, coords, w1, b1, w2, b2, out):
             for c in range(3):
                 nc.scalar.activation(
                     out=sq[:, c, b, :], in_=xbc[:, b, :, c], func=ACT.Square,
-                    bias=xj[:, b, c:c + 1], scale=-1.0,
+                    bias=xj0[:, 0, c:c + 1] if b == 0 else xjr[:, b - 1, c:c + 1], scale=-1.0,
                 )
 
         def add_first(b):
@@ -142,24 +143,13 @@ def tile_distancerelativebias_kernel(tc, coords, w1, b1, w2, b2, out):
         def add_last(b):
             nc.vector.tensor_tensor(out=ssum[:, b, :], in0=ssum[:, b, :], in1=sq[:, 2, b, :], op=ALU.add)
 
-        diff = const.tile([P, 3, N], F32)
-        xjf = const.tile([P, 3], F32)
-        nc.vector.tensor_copy(out=xjf[:], in_=xj[:, LAST, :])
-        for c in range(3):
-            nc.vector.tensor_scalar(
-                out=diff[:, c, :], in0=xbc[:, LAST, :, c], scalar1=xjf[:, c:c + 1], scalar2=None, op0=ALU.subtract,
-            )
-        for b in range(LAST):
+        for b in range(B):
             squares(b)
-        add_first(0)
-        nc.vector.tensor_tensor(out=sq[:, :, LAST, :], in0=diff[:], in1=diff[:], op=ALU.mult)
-        add_last(0)
-        add_first(1)
-        add_first(LAST)
-        add_last(1)
+        for b in range(B):
+            add_first(b)
+            if b > 0:
+                add_last(b - 1)
         add_last(LAST)
-        add_first(2)
-        add_last(2)
         nc.scalar.activation(out=dist[:, 0, :], in_=ssum[:, 0, :], func=ACT.Sqrt)
         nc.scalar.activation(out=dist[:, 1:B, :], in_=ssum[:, 1:B, :], func=ACT.Sqrt)
         nc.vector.tensor_copy(out=w1f[:], in_=w1b[:])
@@ -217,6 +207,7 @@ def tile_distancerelativebias_kernel(tc, coords, w1, b1, w2, b2, out):
         obanks = {}
         otiles = {}
         done = [set() for b in range(B)]
+        copied = [set() for b in range(B)]
         stored = [0 for b in range(B)]
 
         def prep_key(s):
@@ -395,6 +386,7 @@ def tile_distancerelativebias_kernel(tc, coords, w1, b1, w2, b2, out):
                     otiles[b] = opool.tile([P, N * N], F32, name="ot")
                 ov = otiles[b][:].rearrange("p (i j) -> p i j", j=N)
                 i0 = ROWS * g
+                copied[b].add(g)
                 if on_scalar(b, g):
                     nc.scalar.activation(
                         out=ov[:, i0:i0 + ROWS, i0:N], in_=orn[:, :, base:base + N - i0],
@@ -419,9 +411,9 @@ def tile_distancerelativebias_kernel(tc, coords, w1, b1, w2, b2, out):
                 done[b].add(g)
             for b in sorted(set([seg[0] for seg in segments])):
                 complete = stored[b]
-                while complete < GROUPS and complete in done[b]:
+                while complete < GROUPS and complete in copied[b] and (complete == 0 or complete - 1 in done[b]):
                     complete += 1
-                chunk = 2 if (b == LAST and stored[b] >= HALF) else 4
+                chunk = 1 if (b == LAST and stored[b] >= GROUPS // 4) else 4
                 while complete - stored[b] >= chunk:
                     g0 = stored[b]
                     g1 = min(complete, g0 + 4)

@@ -30,7 +30,6 @@ NG = 3
 NQ = 2
 PARTS = 3
 PRODUCT_GROUPS = (6, 14)
-PRODUCT_LEAD = 5
 AHEAD = 2
 LAG_DIRECT = 4
 TAIL_PREP_AT = 18
@@ -105,23 +104,34 @@ def tile_distancerelativebias_kernel(tc, coords, w1, b1, w2, b2, out):
         b2b = const.tile([P, 1], BF16)
         nc.sync.dma_start(out=b2b[:], in_=b2.rearrange("(p o) -> p o", o=1))
 
+        one = const.tile([P, 1], F32)
+        nc.vector.memset(one[:], 1.0)
+        warm = const.tile([P, 1], F32)
+        nc.scalar.activation(out=warm[:], in_=one[:], func=ACT.Sqrt)
+
         izz = const.tile([P, 3 * P], F32)
         nc.gpsimd.memset(izz[:], 0.0)
         make_identity(nc, izz[:, P:2 * P], nomemset=True)
         ident = izz[:, P:2 * P]
 
         mask = const.tile([P, B, N], F32)
-        nc.gpsimd.memset(mask[:], 1.0)
+        nc.vector.memset(mask[:], 1.0)
         nc.gpsimd.affine_select(
             out=mask[:].rearrange("p b i -> p (b i)"), in_=mask[:].rearrange("p b i -> p (b i)"),
             pattern=[[0, B], [-ROWS, GROUPS], [0, ROWS]], compare_op=ALU.is_ge, fill=0.0,
             base=0, channel_multiplier=1,
         )
 
-        one = const.tile([P, 1], F32)
-        nc.vector.memset(one[:], 1.0)
-        warm = const.tile([P, 1], F32)
-        nc.scalar.activation(out=warm[:], in_=one[:], func=ACT.Sqrt)
+        wsel = const.tile([P, ROWS, HID], BF16)
+        nc.vector.memset(wsel[:].rearrange("p r c -> p (r c)").bitcast(I32), 0)
+        for r in range(ROWS):
+            nc.sync.dma_start(
+                out=wsel[PARTS * r:PARTS * (r + 1), r, :], in_=w1.rearrange("o c -> (o c)").partition_broadcast(PARTS)
+            )
+            nc.sync.dma_start(out=wsel[P - 1:P, r, :], in_=b1.rearrange("(o c) -> o c", o=1))
+        parts = const.tile([P, B, 2, P], BF16)
+        nc.vector.memset(parts[:].rearrange("p b k m -> p (b k m)").bitcast(I32), 0)
+        nc.vector.memset(parts[:, :, :, P - 1:P], 1.0)
 
         sq = const.tile([P, 3, B, N], F32)
         ssum = const.tile([P, B, N], F32)
@@ -169,6 +179,8 @@ def tile_distancerelativebias_kernel(tc, coords, w1, b1, w2, b2, out):
         vm = const.tile([P, 2, ROWS], F32)
         vt = const.tile([P, n_tail, ROWS], F32)
 
+        identb = const.tile([P, P], BF16)
+        nc.vector.tensor_copy(out=identb[:], in_=ident)
         w2g = const.tile([P, HEADS, PACK], BF16, align_bytes=64)
         w2c = const.tile([P, HEADS], U32, align_bytes=64)
         w2s = const.tile([P, HEADS], U8, align_bytes=64)
@@ -182,23 +194,10 @@ def tile_distancerelativebias_kernel(tc, coords, w1, b1, w2, b2, out):
         codess = [const.tile([P, UNIT * BANK], U32, name="codes%d" % k, align_bytes=64) for k in range(NQ)]
         scaless = [const.tile([P, UNIT * BANK], U8, name="scales%d" % k, align_bytes=64) for k in range(NQ)]
 
-        wsel = const.tile([P, ROWS, HID], BF16)
-        nc.gpsimd.memset(wsel[:].rearrange("p r c -> p (r c)").bitcast(I32), 0)
-        for r in range(ROWS):
-            nc.sync.dma_start(
-                out=wsel[PARTS * r:PARTS * (r + 1), r, :], in_=w1.rearrange("o c -> (o c)").partition_broadcast(PARTS)
-            )
-            nc.sync.dma_start(out=wsel[P - 1:P, r, :], in_=b1.rearrange("(o c) -> o c", o=1))
-        identb = const.tile([P, P], BF16)
-        nc.gpsimd.tensor_copy(out=identb[:], in_=ident)
-        parts = {}
         drows = {}
         for g in PRODUCT_GROUPS:
-            parts[g] = const.tile([P, B, P], BF16, name="parts%d" % g)
             drows[g] = const.tile([P, B, P], BF16, name="drow%d" % g)
-            nc.gpsimd.memset(parts[g][:].rearrange("p b m -> p (b m)").bitcast(I32), 0)
-            nc.gpsimd.memset(parts[g][:, :, P - 1:P], 1.0)
-        rests = [const.tile([P, B, ROWS], F32, name="rest%d" % e) for e in range(PARTS - 1)]
+        rests = [const.tile([P, B, 2, ROWS], F32, name="rest%d" % e) for e in range(PARTS - 1)]
 
         plans = bank_plans()
         n_banks = len(plans)
@@ -264,18 +263,20 @@ def tile_distancerelativebias_kernel(tc, coords, w1, b1, w2, b2, out):
             kind, key = plans[s][0:2]
             return key[1] if kind in ("pair", "solo") and key[1] in PRODUCT_GROUPS else None
 
-        def split(g):
-            rest = vs[:, :, ROWS * g:ROWS * g + ROWS]
-            pieces = parts[g][:, :, 0:PARTS * ROWS].rearrange("p b (r e) -> p b r e", e=PARTS)
-            for e in range(PARTS):
-                nc.gpsimd.tensor_copy(out=pieces[:, :, :, e], in_=rest)
-                if e + 1 < PARTS:
-                    nc.gpsimd.tensor_tensor(out=rests[e][:], in0=rest, in1=pieces[:, :, :, e], op=ALU.subtract)
-                    rest = rests[e][:]
+        def split(e):
+            i0 = ROWS * PRODUCT_GROUPS[0]
+            merged = vs[:].rearrange("p b (k i) -> p b k i", k=2)[:, :, :, i0:i0 + ROWS]
+            pieces = parts[:, :, :, 0:PARTS * ROWS].rearrange("p b k (r e) -> p b k r e", e=PARTS)
+            left = merged
+            if e > 0:
+                before = rests[e - 2][:] if e > 1 else merged
+                nc.vector.tensor_tensor(out=rests[e - 1][:], in0=before, in1=pieces[:, :, :, :, e - 1], op=ALU.subtract)
+                left = rests[e - 1][:]
+            nc.vector.tensor_copy(out=pieces[:, :, :, :, e], in_=left)
 
         def turn(g):
             for b in range(B):
-                nc.tensor.transpose(vrow[:, b, :], parts[g][:, b, :], identb[:])
+                nc.tensor.transpose(vrow[:, b, :], parts[:, b, PRODUCT_GROUPS.index(g), :], identb[:])
 
         def product(s, rows):
             kind, key, segments, lo, hi = plans[s]
@@ -447,9 +448,8 @@ def tile_distancerelativebias_kernel(tc, coords, w1, b1, w2, b2, out):
                 spread(q)
             if s + AHEAD + 2 < n_banks:
                 pks.append(prep_tensor(s + AHEAD + 2))
-            for g in PRODUCT_GROUPS:
-                if s + PRODUCT_LEAD == first_use[g]:
-                    pks.append(prep_tensor(first_use[g]))
+            if s < len(PRODUCT_GROUPS):
+                pks.append(prep_tensor(first_use[PRODUCT_GROUPS[s]]))
             if s < n_banks:
                 hidden(s)
             if s + 1 < n_banks and product_group(s + 1) is not None:
@@ -475,13 +475,13 @@ def tile_distancerelativebias_kernel(tc, coords, w1, b1, w2, b2, out):
                     mirror_and_store(q)
             for pk in pks:
                 prep_vector(pk)
-            for g in PRODUCT_GROUPS:
-                if s + PRODUCT_LEAD == first_use[g]:
-                    split(g)
-                if s + PRODUCT_LEAD - 1 == first_use[g]:
-                    turn(g)
-                if s + PRODUCT_LEAD - 2 == first_use[g]:
-                    nc.vector.tensor_copy(
-                        out=drows[g][:].rearrange("p b j -> p (b j)"), in_=vrow.rearrange("p b j -> p (b j)")
-                    )
+            if 1 <= s < 1 + PARTS:
+                split(s - 1)
+            if 0 <= s - PARTS - 1 < len(PRODUCT_GROUPS):
+                g = PRODUCT_GROUPS[s - PARTS - 1]
+                nc.vector.tensor_copy(
+                    out=drows[g][:].rearrange("p b j -> p (b j)"), in_=vrow.rearrange("p b j -> p (b j)")
+                )
+            if 0 <= s - PARTS < len(PRODUCT_GROUPS):
+                turn(PRODUCT_GROUPS[s - PARTS])
         assert stored == [GROUPS for b in range(B)]

@@ -406,8 +406,8 @@ def tile_distancerelativebias_kernel(tc, coords, w1, b1, w2, b2, out):
                 i0 = ROWS * g
                 if i0 + ROWS < N:
                     nc.vector.tensor_copy(
-                        out=ov[:, i0 + ROWS:N, i0:i0 + ROWS],
-                        in_=ov[:, i0:i0 + ROWS, i0 + ROWS:N].rearrange("p r j -> p j r"),
+                        out=ov[:, i0 + ROWS:N, i0:i0 + ROWS].rearrange("p (j e) r -> p j r e", e=2),
+                        in_=ov[:, i0:i0 + ROWS, i0 + ROWS:N].rearrange("p r (j e) -> p j r e", e=2),
                     )
                 done[b].add(g)
             for b in sorted(set([seg[0] for seg in segments])):

@@ -23,6 +23,7 @@ ROWS = 4
 GROUPS = N // ROWS
 HALF = GROUPS // 2
 LAST = B - 1
+LATE = 2
 TAIL_SETS = [[17, 18], [19, 20], [21, 22, 23], [24, 25, 26, 27], [28, 29, 30, 31]]
 UNIT = 2
 NUNIT = 3
@@ -42,7 +43,7 @@ PINNED = True
 def on_scalar(b, g):
     if b == LAST:
         return g > HALF or g % 2 == 0
-    return g % 4 == 0
+    return g % 4 == 0 and (b >= LATE or g not in (12, 20, 28))
 
 
 def bank_plans():
@@ -207,6 +208,8 @@ def tile_distancerelativebias_kernel(tc, coords, w1, b1, w2, b2, out):
         otiles = {}
         done = [set() for b in range(B)]
         copied = [set() for b in range(B)]
+        due = []
+        sizes = {}
         stored = [0 for b in range(B)]
 
         def prep_key(s):
@@ -384,8 +387,8 @@ def tile_distancerelativebias_kernel(tc, coords, w1, b1, w2, b2, out):
             ordered.extend([seg for seg in segments if on_scalar(seg[0], seg[1])])
             for (b, g, base) in ordered:
                 if b not in otiles:
-                    otiles[b] = opool.tile([P, N * N], F32, name="ot")
-                ov = otiles[b][:].rearrange("p (i j) -> p i j", j=N)
+                    otiles[b] = opool.tile([P, N * N + N], F32, name="ot")
+                ov = otiles[b][:, 0:N * N].rearrange("p (i j) -> p i j", j=N)
                 i0 = ROWS * g
                 copied[b].add(g)
                 if on_scalar(b, g):
@@ -399,30 +402,56 @@ def tile_distancerelativebias_kernel(tc, coords, w1, b1, w2, b2, out):
                         scalar1=b2f[:, 0:1], scalar2=None, op0=ALU.add,
                     )
 
+        def mirror_rows(b, i0, i1, j0):
+            ov = otiles[b][:, 0:N * N].rearrange("p (i j) -> p i j", j=N)
+            nc.vector.tensor_copy(
+                out=ov[:, j0:N, i0:i1].rearrange("p (j e) (h r) -> p h j r e", e=2, r=ROWS),
+                in_=ov[:, i0:i1, j0:N].rearrange("p (h r) (j e) -> p h j r e", e=2, r=ROWS),
+            )
+
+        def mirror_blocks(b, size):
+            x = 2 * size * (N + 1)
+            blocks = otiles[b][:, 0:N // (2 * size) * x].rearrange("p (u x) -> p u x", x=x)
+            right = blocks[:, :, 0:size * N].rearrange("p u (i c) -> p u i c", c=N)[:, :, :, size:2 * size]
+            below = blocks[:, :, size * N:2 * size * N].rearrange("p u (j c) -> p u j c", c=N)[:, :, :, 0:size]
+            nc.vector.tensor_copy(
+                out=below.rearrange("p u j (h r) -> p u h j r", r=ROWS),
+                in_=right.rearrange("p u (h r) j -> p u h j r", r=ROWS),
+            )
+
+        def store_rows(b, g0, g1):
+            nc.sync.dma_start(
+                out=out[b].rearrange("k i j -> k (i j)")[:, g0 * ROWS * N:g1 * ROWS * N],
+                in_=otiles[b][:, g0 * ROWS * N:g1 * ROWS * N],
+            )
+            stored[b] = g1
+
         def mirror_and_store(s):
-            kind, key, segments, lo, hi = plans[s]
-            for (b, g, base) in segments:
-                ov = otiles[b][:].rearrange("p (i j) -> p i j", j=N)
-                i0 = ROWS * g
-                if i0 + ROWS < N:
-                    nc.vector.tensor_copy(
-                        out=ov[:, i0 + ROWS:N, i0:i0 + ROWS].rearrange("p (j e) r -> p j r e", e=2),
-                        in_=ov[:, i0:i0 + ROWS, i0 + ROWS:N].rearrange("p r (j e) -> p j r e", e=2),
-                    )
-                done[b].add(g)
-            for b in sorted(set([seg[0] for seg in segments])):
+            for (b, g, base) in plans[s][2]:
+                if b >= LATE:
+                    if ROWS * (g + 1) < N:
+                        mirror_rows(b, ROWS * g, ROWS * (g + 1), ROWS * (g + 1))
+                    done[b].add(g)
+            for b in range(LATE, B):
                 complete = stored[b]
                 while complete < GROUPS and complete in copied[b] and (complete == 0 or complete - 1 in done[b]):
                     complete += 1
                 chunk = 1 if (b == LAST and stored[b] >= GROUPS // 4) else 4
                 while complete - stored[b] >= chunk:
-                    g0 = stored[b]
-                    g1 = min(complete, g0 + 4)
-                    nc.sync.dma_start(
-                        out=out[b].rearrange("k i j -> k (i j)")[:, g0 * ROWS * N:g1 * ROWS * N],
-                        in_=otiles[b][:, g0 * ROWS * N:g1 * ROWS * N],
-                    )
-                    stored[b] = g1
+                    store_rows(b, stored[b], min(complete, stored[b] + 4))
+
+        def mirror_unit(u):
+            for b in range(LATE):
+                groups = sorted([g for q in members(u) for (bb, g, base) in plans[q][2] if bb == b])
+                if not groups:
+                    continue
+                upper = [g for g in groups if g < HALF]
+                if upper:
+                    mirror_rows(b, ROWS * upper[0], ROWS * (upper[-1] + 1), N // 2)
+                for g in groups:
+                    done[b].add(g)
+                if len(done[b]) == GROUPS:
+                    due.append(b)
 
         first_use = {}
         for s in range(n_banks):
@@ -470,9 +499,20 @@ def tile_distancerelativebias_kernel(tc, coords, w1, b1, w2, b2, out):
                 shift_tail(*tail_shifts[s - TAIL_PREP_AT])
             if s - TAIL_PREP_AT == len(tail_shifts):
                 nc.vector.tensor_copy(out=vt[:], in_=vtail[:, :, :])
+            for b in range(LATE):
+                if b in due:
+                    size = sizes.get(b, N // 4)
+                    mirror_blocks(b, size)
+                    sizes[b] = size // 2
+                    if size == ROWS:
+                        due.remove(b)
+                        for g in range(0, GROUPS, 4):
+                            store_rows(b, g, g + 4)
             for q in range(max(0, s - LAG_DIRECT - 1), min(n_banks, s)):
                 if direct_step(q) + 1 == s:
                     mirror_and_store(q)
+                    if ends_unit(q):
+                        mirror_unit(unit_of[q])
             for pk in pks:
                 prep_vector(pk)
             if 1 <= s < 1 + PARTS:

@@ -84,8 +84,8 @@ def tile_distancerelativebias_kernel(tc, coords, w1, b1, w2, b2, out):
         const = ctx.enter_context(tc.tile_pool(name="const", bufs=1))
         opool = ctx.enter_context(tc.tile_pool(name="opool", bufs=2))
         vps = ctx.enter_context(tc.psum_pool(name="vps", bufs=1))
-        dps = ctx.enter_context(tc.psum_pool(name="dps", bufs=4))
-        ops = ctx.enter_context(tc.psum_pool(name="ops", bufs=3))
+        dps = ctx.enter_context(tc.psum_pool(name="dps", bufs=5))
+        ops = ctx.enter_context(tc.psum_pool(name="ops", bufs=2))
 
         xj0 = const.tile([P, 1, 3], BF16)
         xjr = const.tile([P, B - 1, 3], BF16)
@@ -470,7 +470,7 @@ def tile_distancerelativebias_kernel(tc, coords, w1, b1, w2, b2, out):
             prep_vector(prep_tensor(s))
         for s in range(n_banks + LAG_DIRECT + 1):
             pks = []
-            for lead, rows in ((1, (2,)), (2, (0, 1))):
+            for lead, rows in ((1, (3,)), (2, (0, 1, 2))):
                 if s + lead < n_banks and product_group(s + lead) is not None:
                     product(s + lead, rows)
             for q in spread_at.get(s, []):
@@ -482,9 +482,8 @@ def tile_distancerelativebias_kernel(tc, coords, w1, b1, w2, b2, out):
             if s < n_banks:
                 hidden(s)
             if s + 1 < n_banks and product_group(s + 1) is not None:
-                product(s + 1, (3,))
+                spread(s + 2)
             if s < n_banks and product_group(s) is not None:
-                spread(s + 1)
                 spread(s + 2)
             if ends_unit(s - 1):
                 regroup(unit_of[s - 1])

@@ -30,7 +30,7 @@ NUNIT = 3
 NG = 3
 NQ = 2
 PARTS = 3
-PRODUCT_GROUPS = (6, 14)
+PRODUCT_GROUPS = (7, 15)
 AHEAD = 2
 LAG_DIRECT = 4
 TAIL_PREP_AT = 18
@@ -43,7 +43,7 @@ PINNED = True
 def on_scalar(b, g):
     if b == LAST:
         return g > HALF or g % 2 == 0
-    return g % 4 == 0 and (b >= LATE or g not in (12, 20, 28))
+    return g % 4 == 0 and (b > 0 or g >= HALF)
 
 
 def bank_plans():
@@ -468,6 +468,7 @@ def tile_distancerelativebias_kernel(tc, coords, w1, b1, w2, b2, out):
             spread(s)
         for s in range(AHEAD + 2):
             prep_vector(prep_tensor(s))
+        waiting = [prep_tensor(AHEAD + 2)]
         for s in range(n_banks + LAG_DIRECT + 1):
             pks = []
             for lead, rows in ((1, (3,)), (2, (0, 1, 2))):
@@ -475,8 +476,8 @@ def tile_distancerelativebias_kernel(tc, coords, w1, b1, w2, b2, out):
                     product(s + lead, rows)
             for q in spread_at.get(s, []):
                 spread(q)
-            if s + AHEAD + 2 < n_banks:
-                pks.append(prep_tensor(s + AHEAD + 2))
+            if s + AHEAD + 3 < n_banks:
+                pks.append(prep_tensor(s + AHEAD + 3))
             if s < len(PRODUCT_GROUPS):
                 pks.append(prep_tensor(first_use[PRODUCT_GROUPS[s]]))
             if s < n_banks:
@@ -512,15 +513,16 @@ def tile_distancerelativebias_kernel(tc, coords, w1, b1, w2, b2, out):
                     mirror_and_store(q)
                     if ends_unit(q):
                         mirror_unit(unit_of[q])
-            for pk in pks:
+            for pk in waiting:
                 prep_vector(pk)
-            if 1 <= s < 1 + PARTS:
-                split(s - 1)
-            if 0 <= s - PARTS - 1 < len(PRODUCT_GROUPS):
-                g = PRODUCT_GROUPS[s - PARTS - 1]
-                nc.vector.tensor_copy(
-                    out=drows[g][:].rearrange("p b j -> p (b j)"), in_=vrow.rearrange("p b j -> p (b j)")
-                )
-            if 0 <= s - PARTS < len(PRODUCT_GROUPS):
-                turn(PRODUCT_GROUPS[s - PARTS])
+            waiting = pks
+            if 2 <= s < 2 + PARTS:
+                split(s - 2)
+            for k, g in enumerate(PRODUCT_GROUPS):
+                if s == 1 + PARTS + 4 * k:
+                    turn(g)
+                if s == 2 + PARTS + 4 * k:
+                    nc.vector.tensor_copy(
+                        out=drows[g][:].rearrange("p b j -> p (b j)"), in_=vrow.rearrange("p b j -> p (b j)")
+                    )
         assert stored == [GROUPS for b in range(B)]

@@ -29,8 +29,11 @@ UNIT = 2
 NUNIT = 3
 NG = 3
 NQ = 2
+PRODUCT_PREP = 5
+SPLIT_AT = 9
 PARTS = 3
-PRODUCT_GROUPS = (7, 15)
+PRODUCT_GROUPS = (6, 10, 14)
+PRODUCT_PLANS = ((0, 14), (1, 6), (1, 10), (1, 14), (2, 6), (2, 10), (2, 14), (3, 10))
 AHEAD = 2
 LAG_DIRECT = 4
 TAIL_PREP_AT = 18
@@ -43,7 +46,7 @@ PINNED = True
 def on_scalar(b, g):
     if b == LAST:
         return g > HALF or g % 2 == 0
-    return g % 4 == 0 and (b > 0 or g >= HALF)
+    return g % 4 == 0 and (b > 0 or g >= 8)
 
 
 def bank_plans():
@@ -90,16 +93,16 @@ def tile_distancerelativebias_kernel(tc, coords, w1, b1, w2, b2, out):
         xj0 = const.tile([P, 1, 3], BF16)
         xjr = const.tile([P, B - 1, 3], BF16)
         xbc = const.tile([P, B, N, 3], BF16)
+        w1b = const.tile([P, PACK], BF16)
+        b1b = const.tile([P, PACK], BF16)
         for part, xj in ((slice(0, 1), xj0), (slice(1, B), xjr)):
             nc.scalar.dma_start(out=xj[:], in_=coords[part].rearrange("b j c -> j b c"))
             nc.sync.dma_start(
                 out=xbc[:, part].rearrange("p b i c -> p (b i c)"),
                 in_=coords[part].rearrange("b i c -> (b i c)").partition_broadcast(P),
             )
-        w1b = const.tile([P, PACK], BF16)
-        nc.sync.dma_start(out=w1b[:], in_=w1.rearrange("o (p t) -> (o p) t", t=PACK))
-        b1b = const.tile([P, PACK], BF16)
-        nc.sync.dma_start(out=b1b[:], in_=b1.rearrange("(p t) -> p t", t=PACK))
+        nc.scalar.dma_start(out=w1b[:], in_=w1.rearrange("o (p t) -> (o p) t", t=PACK))
+        nc.scalar.dma_start(out=b1b[:], in_=b1.rearrange("(p t) -> p t", t=PACK))
         w2b = const.tile([P, PACK, HEADS], BF16)
         nc.sync.dma_start(out=w2b[:], in_=w2.rearrange("(p t) m -> p t m", t=PACK))
         b2b = const.tile([P, 1], BF16)
@@ -115,11 +118,10 @@ def tile_distancerelativebias_kernel(tc, coords, w1, b1, w2, b2, out):
         make_identity(nc, izz[:, P:2 * P], nomemset=True)
         ident = izz[:, P:2 * P]
 
-        mask = const.tile([P, B, N], F32)
+        mask = const.tile([P, 1, N], F32)
         nc.vector.memset(mask[:], 1.0)
         nc.gpsimd.affine_select(
-            out=mask[:].rearrange("p b i -> p (b i)"), in_=mask[:].rearrange("p b i -> p (b i)"),
-            pattern=[[0, B], [-ROWS, GROUPS], [0, ROWS]], compare_op=ALU.is_ge, fill=0.0,
+            out=mask[:, 0, :], in_=mask[:, 0, :], pattern=[[-ROWS, GROUPS], [0, ROWS]], compare_op=ALU.is_ge, fill=0.0,
             base=0, channel_multiplier=1,
         )
 
@@ -130,7 +132,7 @@ def tile_distancerelativebias_kernel(tc, coords, w1, b1, w2, b2, out):
                 out=wsel[PARTS * r:PARTS * (r + 1), r, :], in_=w1.rearrange("o c -> (o c)").partition_broadcast(PARTS)
             )
             nc.sync.dma_start(out=wsel[P - 1:P, r, :], in_=b1.rearrange("(o c) -> o c", o=1))
-        parts = const.tile([P, B, 2, P], BF16)
+        parts = const.tile([P, B, len(PRODUCT_GROUPS), P], BF16)
         nc.vector.memset(parts[:].rearrange("p b k m -> p (b k m)").bitcast(I32), 0)
         nc.vector.memset(parts[:, :, :, P - 1:P], 1.0)
 
@@ -163,12 +165,11 @@ def tile_distancerelativebias_kernel(tc, coords, w1, b1, w2, b2, out):
         add_last(LAST)
         nc.scalar.activation(out=dist[:, 0, :], in_=ssum[:, 0, :], func=ACT.Sqrt)
         nc.scalar.activation(out=dist[:, 1:B, :], in_=ssum[:, 1:B, :], func=ACT.Sqrt)
-        nc.vector.tensor_copy(out=w1f[:], in_=w1b[:])
-        nc.vector.tensor_copy(out=b1f[:], in_=b1b[:])
-        nc.vector.tensor_copy(out=b2f[:], in_=b2b[:])
 
         dm = const.tile([P, B, N], F32)
-        nc.vector.tensor_tensor(out=dm[:], in0=dist[:], in1=mask[:], op=ALU.mult)
+        nc.vector.tensor_copy(out=w1f[:], in_=w1b[:])
+        nc.vector.tensor_copy(out=b1f[:], in_=b1b[:])
+        nc.vector.tensor_tensor(out=dm[:], in0=dist[:], in1=mask[:].to_broadcast([P, B, N]), op=ALU.mult)
         dmk = dm[:].rearrange("p (k e) i -> p k e i", e=2)
         n_tail = len(TAIL_SETS)
         vp = vps.tile([P, BANK], F32)
@@ -181,14 +182,9 @@ def tile_distancerelativebias_kernel(tc, coords, w1, b1, w2, b2, out):
         vt = const.tile([P, n_tail, ROWS], F32)
 
         identb = const.tile([P, P], BF16)
-        nc.vector.tensor_copy(out=identb[:], in_=ident)
         w2g = const.tile([P, HEADS, PACK], BF16, align_bytes=64)
         w2c = const.tile([P, HEADS], U32, align_bytes=64)
         w2s = const.tile([P, HEADS], U8, align_bytes=64)
-        nc.vector.tensor_copy(out=w2g[:], in_=w2b[:].rearrange("p t m -> p m t"))
-        nc.vector.quantize_mx(
-            out=w2c[:].bitcast(FP8X4), scales=w2s[:], in_=w2g[:].rearrange("p m t -> p (m t)")
-        )
 
         hts = [const.tile([P, PACK, UNIT * BANK], BF16, name="ht%d" % k) for k in range(NUNIT)]
         groupeds = [const.tile([P, UNIT * BANK, PACK], BF16, name="grouped%d" % k, align_bytes=64) for k in range(NG)]
@@ -198,7 +194,7 @@ def tile_distancerelativebias_kernel(tc, coords, w1, b1, w2, b2, out):
         drows = {}
         for g in PRODUCT_GROUPS:
             drows[g] = const.tile([P, B, P], BF16, name="drow%d" % g)
-        rests = [const.tile([P, B, 2, ROWS], F32, name="rest%d" % e) for e in range(PARTS - 1)]
+        rests = [const.tile([P, B, len(PRODUCT_GROUPS), ROWS], F32, name="rest%d" % e) for e in range(PARTS - 1)]
 
         plans = bank_plans()
         n_banks = len(plans)
@@ -264,11 +260,10 @@ def tile_distancerelativebias_kernel(tc, coords, w1, b1, w2, b2, out):
 
         def product_group(s):
             kind, key = plans[s][0:2]
-            return key[1] if kind in ("pair", "solo") and key[1] in PRODUCT_GROUPS else None
+            return key[1] if kind in ("pair", "solo") and key in PRODUCT_PLANS else None
 
         def split(e):
-            i0 = ROWS * PRODUCT_GROUPS[0]
-            merged = vs[:].rearrange("p b (k i) -> p b k i", k=2)[:, :, :, i0:i0 + ROWS]
+            merged = vs[:].rearrange("p b (k i) -> p b k i", i=4 * ROWS)[:, :, 1:4, 2 * ROWS:3 * ROWS]
             pieces = parts[:, :, :, 0:PARTS * ROWS].rearrange("p b k (r e) -> p b k r e", e=PARTS)
             left = merged
             if e > 0:
@@ -325,8 +320,8 @@ def tile_distancerelativebias_kernel(tc, coords, w1, b1, w2, b2, out):
                 )
 
         units = [[0], [1]]
-        units.extend([[q, q + 1] for q in range(2, n_banks - n_tail, UNIT)])
-        units.extend([[q] for q in range(n_banks - n_tail, n_banks)])
+        units.extend([[q, q + 1] for q in range(2, n_banks - n_tail - 2, UNIT)])
+        units.extend([[q] for q in range(n_banks - n_tail - 2, n_banks)])
         unit_of = {}
         for u, plan_list in enumerate(units):
             for q in plan_list:
@@ -346,6 +341,8 @@ def tile_distancerelativebias_kernel(tc, coords, w1, b1, w2, b2, out):
 
         def regroup(u):
             plain = [q for q in members(u) if product_group(q) is None]
+            if not plain:
+                return
             lo = min([plans[q][3] for q in plain])
             hi = max([plans[q][4] for q in plain])
             first = place(plain[0])[1]
@@ -468,9 +465,15 @@ def tile_distancerelativebias_kernel(tc, coords, w1, b1, w2, b2, out):
             spread(s)
         for s in range(AHEAD + 2):
             prep_vector(prep_tensor(s))
-        waiting = [prep_tensor(AHEAD + 2)]
+        nc.vector.tensor_copy(out=w2g[:], in_=w2b[:].rearrange("p t m -> p m t"))
+        nc.vector.quantize_mx(
+            out=w2c[:].bitcast(FP8X4), scales=w2s[:], in_=w2g[:].rearrange("p m t -> p (m t)")
+        )
+        nc.vector.tensor_copy(out=b2f[:], in_=b2b[:])
+        nc.vector.tensor_copy(out=identb[:], in_=ident)
+        waiting = []
+        pks = [prep_tensor(AHEAD + 2)]
         for s in range(n_banks + LAG_DIRECT + 1):
-            pks = []
             for lead, rows in ((1, (3,)), (2, (0, 1, 2))):
                 if s + lead < n_banks and product_group(s + lead) is not None:
                     product(s + lead, rows)
@@ -478,8 +481,8 @@ def tile_distancerelativebias_kernel(tc, coords, w1, b1, w2, b2, out):
                 spread(q)
             if s + AHEAD + 3 < n_banks:
                 pks.append(prep_tensor(s + AHEAD + 3))
-            if s < len(PRODUCT_GROUPS):
-                pks.append(prep_tensor(first_use[PRODUCT_GROUPS[s]]))
+            if s == PRODUCT_PREP:
+                pks.append(prep_tensor(first_use[PRODUCT_GROUPS[-1]]))
             if s < n_banks:
                 hidden(s)
             if s + 1 < n_banks and product_group(s + 1) is not None:
@@ -516,12 +519,13 @@ def tile_distancerelativebias_kernel(tc, coords, w1, b1, w2, b2, out):
             for pk in waiting:
                 prep_vector(pk)
             waiting = pks
-            if 2 <= s < 2 + PARTS:
-                split(s - 2)
-            for k, g in enumerate(PRODUCT_GROUPS):
-                if s == 1 + PARTS + 4 * k:
+            pks = []
+            if 0 <= s - SPLIT_AT < PARTS:
+                split(s - SPLIT_AT)
+            for k, g in enumerate(reversed(PRODUCT_GROUPS)):
+                if s == SPLIT_AT + PARTS + 2 * k - 1:
                     turn(g)
-                if s == 2 + PARTS + 4 * k:
+                if s == SPLIT_AT + PARTS + 2 * k:
                     nc.vector.tensor_copy(
                         out=drows[g][:].rearrange("p b j -> p (b j)"), in_=vrow.rearrange("p b j -> p (b j)")
                     )

from contextlib import ExitStack

import concourse.mybir as mybir
from concourse.masks import make_identity

F32 = mybir.dt.float32
BF16 = mybir.dt.bfloat16
U32 = mybir.dt.uint32
U8 = mybir.dt.uint8
I32 = mybir.dt.int32
FP8X4 = mybir.dt.float8_e4m3fn_x4
ACT = mybir.ActivationFunctionType
ALU = mybir.AluOpType

P = 128
B = 4
N = 128
HID = 512
HEADS = 128
PACK = 4
BANK = 512
ROWS = 4
GROUPS = N // ROWS
HALF = GROUPS // 2
LAST = B - 1
LATE = 2
TAIL_SETS = [[17, 18], [19, 20], [21, 22, 23], [24, 25, 26, 27], [28, 29, 30, 31]]
UNIT = 2
NUNIT = 3
NG = 3
NQ = 2
PRODUCT_PREP = 5
SPLIT_AT = 9
PARTS = 3
PRODUCT_GROUPS = (6, 10, 14)
PRODUCT_PLANS = ((0, 14), (1, 6), (1, 10), (1, 14), (2, 6), (2, 10), (2, 14), (3, 10))
AHEAD = 2
LAG_DIRECT = 4
TAIL_PREP_AT = 18

FLOPS = 2 * B * N * N * HID * HEADS

PINNED = True


def on_scalar(b, g):
    if b == LAST:
        return g > HALF or g % 2 == 0
    return g % 4 == 0 and (b > 0 or g >= 8)


def bank_plans():
    def solo(b, g):
        return ("solo", (b, g), [(b, g, ROWS * g)], ROWS * g, N)

    def pair(b, g):
        return ("pair", (b, g), [(b, g, ROWS * g), (b, GROUPS - g, 0)], 0, N)

    def mid(k):
        return ("mid", k, [(2 * k, HALF, N // 2), (2 * k + 1, HALF, 0)], 0, N)

    def tail(k):
        segments = []
        base = 0
        for g in TAIL_SETS[k]:
            segments.append((LAST, g, base))
            base += N - ROWS * g
        return ("tail", k, segments, 0, base)

    plans = [solo(0, 0), solo(1, 0)]
    plans.extend([pair(0, g) for g in range(1, HALF)])
    plans.append(mid(0))
    plans.extend([pair(1, g) for g in range(1, HALF)])
    plans.append(solo(2, 0))
    plans.extend([pair(2, g) for g in range(1, HALF)])
    plans.append(mid(1))
    plans.extend([solo(LAST, g) for g in range(HALF)])
    plans.extend([tail(k) for k in range(len(TAIL_SETS))])
    return plans


def tile_distancerelativebias_kernel(tc, coords, w1, b1, w2, b2, out):
    nc = tc.nc
    with ExitStack() as ctx:
        if PINNED:
            ctx.enter_context(tc.manual_schedule())
        const = ctx.enter_context(tc.tile_pool(name="const", bufs=1))
        opool = ctx.enter_context(tc.tile_pool(name="opool", bufs=2))
        vps = ctx.enter_context(tc.psum_pool(name="vps", bufs=1))
        dps = ctx.enter_context(tc.psum_pool(name="dps", bufs=5))
        ops = ctx.enter_context(tc.psum_pool(name="ops", bufs=2))

        xj0 = const.tile([P, 1, 3], BF16)
        xjr = const.tile([P, B - 1, 3], BF16)
        xbc = const.tile([P, B, N, 3], BF16)
        w1b = const.tile([P, PACK], BF16)
        b1b = const.tile([P, PACK], BF16)
        for part, xj in ((slice(0, 1), xj0), (slice(1, B), xjr)):
            nc.scalar.dma_start(out=xj[:], in_=coords[part].rearrange("b j c -> j b c"))
            nc.sync.dma_start(
                out=xbc[:, part].rearrange("p b i c -> p (b i c)"),
                in_=coords[part].rearrange("b i c -> (b i c)").partition_broadcast(P),
            )
        nc.scalar.dma_start(out=w1b[:], in_=w1.rearrange("o (p t) -> (o p) t", t=PACK))
        nc.scalar.dma_start(out=b1b[:], in_=b1.rearrange("(p t) -> p t", t=PACK))
        w2b = const.tile([P, PACK, HEADS], BF16)
        nc.sync.dma_start(out=w2b[:], in_=w2.rearrange("(p t) m -> p t m", t=PACK))
        b2b = const.tile([P, 1], BF16)
        nc.sync.dma_start(out=b2b[:], in_=b2.rearrange("(p o) -> p o", o=1))

        one = const.tile([P, 1], F32)
        nc.vector.memset(one[:], 1.0)
        warm = const.tile([P, 1], F32)
        nc.scalar.activation(out=warm[:], in_=one[:], func=ACT.Sqrt)

        izz = const.tile([P, 3 * P], F32)
        nc.gpsimd.memset(izz[:], 0.0)
        make_identity(nc, izz[:, P:2 * P], nomemset=True)
        ident = izz[:, P:2 * P]

        mask = const.tile([P, 1, N], F32)
        nc.vector.memset(mask[:], 1.0)
        nc.gpsimd.affine_select(
            out=mask[:, 0, :], in_=mask[:, 0, :], pattern=[[-ROWS, GROUPS], [0, ROWS]], compare_op=ALU.is_ge, fill=0.0,
            base=0, channel_multiplier=1,
        )

        wsel = const.tile([P, ROWS, HID], BF16)
        nc.vector.memset(wsel[:].rearrange("p r c -> p (r c)").bitcast(I32), 0)
        for r in range(ROWS):
            nc.sync.dma_start(
                out=wsel[PARTS * r:PARTS * (r + 1), r, :], in_=w1.rearrange("o c -> (o c)").partition_broadcast(PARTS)
            )
            nc.sync.dma_start(out=wsel[P - 1:P, r, :], in_=b1.rearrange("(o c) -> o c", o=1))
        parts = const.tile([P, B, len(PRODUCT_GROUPS), P], BF16)
        nc.vector.memset(parts[:].rearrange("p b k m -> p (b k m)").bitcast(I32), 0)
        nc.vector.memset(parts[:, :, :, P - 1:P], 1.0)

        sq = const.tile([P, 3, B, N], F32)
        ssum = const.tile([P, B, N], F32)
        dist = const.tile([P, B, N], F32)
        w1f = const.tile([P, PACK], F32)
        b1f = const.tile([P, PACK], F32)
        b2f = const.tile([P, 1], F32)

        def squares(b):
            for c in range(3):
                nc.scalar.activation(
                    out=sq[:, c, b, :], in_=xbc[:, b, :, c], func=ACT.Square,
                    bias=xj0[:, 0, c:c + 1] if b == 0 else xjr[:, b - 1, c:c + 1], scale=-1.0,
                )

        def add_first(b):
            nc.vector.tensor_tensor(out=ssum[:, b, :], in0=sq[:, 0, b, :], in1=sq[:, 1, b, :], op=ALU.add)

        def add_last(b):
            nc.vector.tensor_tensor(out=ssum[:, b, :], in0=ssum[:, b, :], in1=sq[:, 2, b, :], op=ALU.add)

        for b in range(B):
            squares(b)
        for b in range(B):
            add_first(b)
            if b > 0:
                add_last(b - 1)
        add_last(LAST)
        nc.scalar.activation(out=dist[:, 0, :], in_=ssum[:, 0, :], func=ACT.Sqrt)
        nc.scalar.activation(out=dist[:, 1:B, :], in_=ssum[:, 1:B, :], func=ACT.Sqrt)

        dm = const.tile([P, B, N], F32)
        nc.vector.tensor_copy(out=w1f[:], in_=w1b[:])
        nc.vector.tensor_copy(out=b1f[:], in_=b1b[:])
        nc.vector.tensor_tensor(out=dm[:], in0=dist[:], in1=mask[:].to_broadcast([P, B, N]), op=ALU.mult)
        dmk = dm[:].rearrange("p (k e) i -> p k e i", e=2)
        n_tail = len(TAIL_SETS)
        vp = vps.tile([P, BANK], F32)
        c_mid = B * (N // 2)
        vpair = vp[:, 0:c_mid].rearrange("p (b i) -> p b i", b=B)
        vtail = vp[:, c_mid:c_mid + n_tail * ROWS].rearrange("p (k r) -> p k r", k=n_tail)
        vrow = vp[:, c_mid:BANK].bitcast(BF16).rearrange("p (b j) -> p b j", b=B)
        vs = const.tile([P, B, N // 2], F32)
        vm = const.tile([P, 2, ROWS], F32)
        vt = const.tile([P, n_tail, ROWS], F32)

        identb = const.tile([P, P], BF16)
        w2g = const.tile([P, HEADS, PACK], BF16, align_bytes=64)
        w2c = const.tile([P, HEADS], U32, align_bytes=64)
        w2s = const.tile([P, HEADS], U8, align_bytes=64)

        hts = [const.tile([P, PACK, UNIT * BANK], BF16, name="ht%d" % k) for k in range(NUNIT)]
        groupeds = [const.tile([P, UNIT * BANK, PACK], BF16, name="grouped%d" % k, align_bytes=64) for k in range(NG)]
        codess = [const.tile([P, UNIT * BANK], U32, name="codes%d" % k, align_bytes=64) for k in range(NQ)]
        scaless = [const.tile([P, UNIT * BANK], U8, name="scales%d" % k, align_bytes=64) for k in range(NQ)]

        drows = {}
        for g in PRODUCT_GROUPS:
            drows[g] = const.tile([P, B, P], BF16, name="drow%d" % g)
        rests = [const.tile([P, B, len(PRODUCT_GROUPS), ROWS], F32, name="rest%d" % e) for e in range(PARTS - 1)]

        plans = bank_plans()
        n_banks = len(plans)
        prepared = set()
        dbanks = {}
        obanks = {}
        otiles = {}
        done = [set() for b in range(B)]
        copied = [set() for b in range(B)]
        due = []
        sizes = {}
        stored = [0 for b in range(B)]

        def prep_key(s):
            kind, key, segments, lo, hi = plans[s]
            if kind == "pair":
                return ("pair", key[1])
            if kind == "mid":
                return ("mid", key)
            return None

        def prep_tensor(s):
            pk = prep_key(s)
            if pk is None or pk in prepared:
                return None
            prepared.add(pk)
            kind, key = pk
            if kind == "pair":
                w = 2 * P - ROWS * key
                i2 = N - ROWS * key
                nc.tensor.matmul(
                    out=vpair[:, :, ROWS * key:ROWS * key + ROWS], lhsT=izz[:, w:w + P],
                    rhs=dm[:, :, i2:i2 + ROWS], start=True, stop=True,
                )
            else:
                nc.tensor.matmul(
                    out=vpair[:, key, 0:ROWS], lhsT=izz[:, P + N // 2:2 * P + N // 2],
                    rhs=dmk[:, key, 1, N // 2:N // 2 + ROWS], start=True, stop=True,
                )
            return pk

        tail_shifts = [(k, q) for k in range(n_tail) for q in range(len(TAIL_SETS[k]))]

        def shift_tail(k, q):
            b, g, base = plans[n_banks - n_tail + k][2][q]
            w = P + ROWS * g - base
            nc.tensor.matmul(
                out=vtail[:, k, :], lhsT=izz[:, w:w + P], rhs=dm[:, b, ROWS * g:ROWS * g + ROWS],
                start=(q == 0), stop=(q == len(TAIL_SETS[k]) - 1),
            )

        def prep_vector(pk):
            if pk is None:
                return
            kind, key = pk
            if kind == "pair":
                cols = slice(ROWS * key, ROWS * key + ROWS)
                nc.vector.tensor_tensor(out=vs[:, :, cols], in0=dm[:, :, cols], in1=vpair[:, :, cols], op=ALU.add)
            else:
                nc.vector.tensor_tensor(
                    out=vm[:, key, :], in0=dmk[:, key, 0, N // 2:N // 2 + ROWS], in1=vpair[:, key, 0:ROWS], op=ALU.add
                )

        def product_group(s):
            kind, key = plans[s][0:2]
            return key[1] if kind in ("pair", "solo") and key in PRODUCT_PLANS else None

        def split(e):
            merged = vs[:].rearrange("p b (k i) -> p b k i", i=4 * ROWS)[:, :, 1:4, 2 * ROWS:3 * ROWS]
            pieces = parts[:, :, :, 0:PARTS * ROWS].rearrange("p b k (r e) -> p b k r e", e=PARTS)
            left = merged
            if e > 0:
                before = rests[e - 2][:] if e > 1 else merged
                nc.vector.tensor_tensor(out=rests[e - 1][:], in0=before, in1=pieces[:, :, :, :, e - 1], op=ALU.subtract)
                left = rests[e - 1][:]
            nc.vector.tensor_copy(out=pieces[:, :, :, :, e], in_=left)

        def turn(g):
            for b in range(B):
                nc.tensor.transpose(vrow[:, b, :], parts[:, b, PRODUCT_GROUPS.index(g), :], identb[:])

        def product(s, rows):
            kind, key, segments, lo, hi = plans[s]
            for r in rows:
                dbanks[s, r] = dps.tile([P, BANK], F32, name="dbank")
                weights = wsel[:, r, :].rearrange("p (m t) -> p t m", t=PACK)
                for t in range(PACK):
                    nc.tensor.matmul(
                        out=dbanks[s, r][:, t * N + lo:t * N + hi], lhsT=weights[:, t, :],
                        rhs=drows[key[1]][:, key[0], lo:hi], start=True, stop=True,
                    )

        def spread(s):
            kind, key, segments, lo, hi = plans[s]
            dbanks[s] = dps.tile([P, BANK], F32, name="dbank")
            for r in range(ROWS):
                if kind == "solo":
                    col = dist[:, key[0], ROWS * key[1] + r:ROWS * key[1] + r + 1]
                elif kind == "pair":
                    col = vs[:, key[0], ROWS * key[1] + r:ROWS * key[1] + r + 1]
                elif kind == "mid":
                    col = vm[:, key, r:r + 1]
                else:
                    col = vt[:, key, r:r + 1]
                nc.tensor.transpose(dbanks[s][:, r * P:(r + 1) * P], col.to_broadcast([P, P]), ident)

        def hidden(s):
            kind, key, segments, lo, hi = plans[s]
            u, half = place(s)
            if product_group(s) is not None:
                for r in range(ROWS):
                    nc.scalar.activation(
                        out=groupeds[u % NG][:, half + r * N + lo:half + r * N + hi, :],
                        in_=dbanks[s, r][:].rearrange("p (t n) -> p n t", t=PACK)[:, lo:hi, :], func=ACT.Silu,
                    )
                return
            ht = hts[u % NUNIT]
            for t in range(PACK):
                nc.scalar.activation(
                    out=ht[:, t, half:half + BANK].rearrange("p (r n) -> p r n", r=ROWS)[:, :, lo:hi],
                    in_=dbanks[s][:].rearrange("p (r n) -> p r n", r=ROWS)[:, :, lo:hi],
                    func=ACT.Silu, bias=b1f[:, t:t + 1], scale=w1f[:, t:t + 1],
                )

        units = [[0], [1]]
        units.extend([[q, q + 1] for q in range(2, n_banks - n_tail - 2, UNIT)])
        units.extend([[q] for q in range(n_banks - n_tail - 2, n_banks)])
        unit_of = {}
        for u, plan_list in enumerate(units):
            for q in plan_list:
                unit_of[q] = u

        def members(u):
            return units[u]

        def ends_unit(s):
            return 0 <= s < n_banks and s == units[unit_of[s]][-1]

        def direct_step(q):
            return q + LAG_DIRECT - (1 if len(units[unit_of[q]]) == 1 else 0)

        def place(s):
            return unit_of[s], (s - units[unit_of[s]][0]) * BANK

        def regroup(u):
            plain = [q for q in members(u) if product_group(q) is None]
            if not plain:
                return
            lo = min([plans[q][3] for q in plain])
            hi = max([plans[q][4] for q in plain])
            first = place(plain[0])[1]
            last = place(plain[-1])[1] + BANK
            ht = hts[u % NUNIT][:, :, first:last]
            grouped = groupeds[u % NG][:, first:last, :]
            if lo == 0 and hi == N:
                nc.vector.tensor_copy(
                    out=grouped.rearrange("p (c i) t -> p c t i", i=4),
                    in_=ht.rearrange("p t (c i) -> p c t i", i=4),
                )
            else:
                nc.vector.tensor_copy(
                    out=grouped.rearrange("p (r c i) t -> p r c t i", c=N // 4, i=4)[:, :, lo // 4:hi // 4],
                    in_=ht.rearrange("p t (r c i) -> p r c t i", c=N // 4, i=4)[:, :, lo // 4:hi // 4],
                )

        def quantise(u):
            width = len(members(u)) * BANK
            nc.vector.quantize_mx(
                out=codess[u % NQ][:, 0:width].bitcast(FP8X4), scales=scaless[u % NQ][:, 0:width],
                in_=groupeds[u % NG][:, 0:width, :].rearrange("p w t -> p (w t)"),
            )

        def multiply(s):
            u, half = place(s)
            obanks[s] = ops.tile([P, BANK], F32, name="obank")
            nc.tensor.matmul_mx(
                out=obanks[s][:], lhsT=w2c[:].bitcast(FP8X4), lhsT_scale=w2s[:],
                rhs=codess[u % NQ][:, half:half + BANK].bitcast(FP8X4),
                rhs_scale=scaless[u % NQ][:, half:half + BANK],
                start=True, stop=True,
            )

        def direct(s):
            kind, key, segments, lo, hi = plans[s]
            orn = obanks[s][:].rearrange("p (r n) -> p r n", r=ROWS)
            ordered = [seg for seg in segments if not on_scalar(seg[0], seg[1])]
            ordered.extend([seg for seg in segments if on_scalar(seg[0], seg[1])])
            for (b, g, base) in ordered:
                if b not in otiles:
                    otiles[b] = opool.tile([P, N * N + N], F32, name="ot")
                ov = otiles[b][:, 0:N * N].rearrange("p (i j) -> p i j", j=N)
                i0 = ROWS * g
                copied[b].add(g)
                if on_scalar(b, g):
                    nc.scalar.activation(
                        out=ov[:, i0:i0 + ROWS, i0:N], in_=orn[:, :, base:base + N - i0],
                        func=ACT.Identity, bias=b2f[:, 0:1], scale=1.0,
                    )
                else:
                    nc.vector.tensor_scalar(
                        out=ov[:, i0:i0 + ROWS, i0:N], in0=orn[:, :, base:base + N - i0],
                        scalar1=b2f[:, 0:1], scalar2=None, op0=ALU.add,
                    )

        def mirror_rows(b, i0, i1, j0):
            ov = otiles[b][:, 0:N * N].rearrange("p (i j) -> p i j", j=N)
            nc.vector.tensor_copy(
                out=ov[:, j0:N, i0:i1].rearrange("p (j e) (h r) -> p h j r e", e=2, r=ROWS),
                in_=ov[:, i0:i1, j0:N].rearrange("p (h r) (j e) -> p h j r e", e=2, r=ROWS),
            )

        def mirror_blocks(b, size):
            x = 2 * size * (N + 1)
            blocks = otiles[b][:, 0:N // (2 * size) * x].rearrange("p (u x) -> p u x", x=x)
            right = blocks[:, :, 0:size * N].rearrange("p u (i c) -> p u i c", c=N)[:, :, :, size:2 * size]
            below = blocks[:, :, size * N:2 * size * N].rearrange("p u (j c) -> p u j c", c=N)[:, :, :, 0:size]
            nc.vector.tensor_copy(
                out=below.rearrange("p u j (h r) -> p u h j r", r=ROWS),
                in_=right.rearrange("p u (h r) j -> p u h j r", r=ROWS),
            )

        def store_rows(b, g0, g1):
            nc.sync.dma_start(
                out=out[b].rearrange("k i j -> k (i j)")[:, g0 * ROWS * N:g1 * ROWS * N],
                in_=otiles[b][:, g0 * ROWS * N:g1 * ROWS * N],
            )
            stored[b] = g1

        def mirror_and_store(s):
            for (b, g, base) in plans[s][2]:
                if b >= LATE:
                    if ROWS * (g + 1) < N:
                        mirror_rows(b, ROWS * g, ROWS * (g + 1), ROWS * (g + 1))
                    done[b].add(g)
            for b in range(LATE, B):
                complete = stored[b]
                while complete < GROUPS and complete in copied[b] and (complete == 0 or complete - 1 in done[b]):
                    complete += 1
                chunk = 1 if (b == LAST and stored[b] >= GROUPS // 4) else 4
                while complete - stored[b] >= chunk:
                    store_rows(b, stored[b], min(complete, stored[b] + 4))

        def mirror_unit(u):
            for b in range(LATE):
                groups = sorted([g for q in members(u) for (bb, g, base) in plans[q][2] if bb == b])
                if not groups:
                    continue
                upper = [g for g in groups if g < HALF]
                if upper:
                    mirror_rows(b, ROWS * upper[0], ROWS * (upper[-1] + 1), N // 2)
                for g in groups:
                    done[b].add(g)
                if len(done[b]) == GROUPS:
                    due.append(b)

        first_use = {}
        for s in range(n_banks):
            if product_group(s) is not None:
                first_use.setdefault(product_group(s), s)
        spread_at = {}
        for s in range(AHEAD, n_banks):
            if product_group(s) is None:
                late = product_group(s - 1) is not None or product_group(s - 2) is not None
                if not late:
                    spread_at.setdefault(s - AHEAD, []).append(s)

        for s in range(AHEAD):
            spread(s)
        for s in range(AHEAD + 2):
            prep_vector(prep_tensor(s))
        nc.vector.tensor_copy(out=w2g[:], in_=w2b[:].rearrange("p t m -> p m t"))
        nc.vector.quantize_mx(
            out=w2c[:].bitcast(FP8X4), scales=w2s[:], in_=w2g[:].rearrange("p m t -> p (m t)")
        )
        nc.vector.tensor_copy(out=b2f[:], in_=b2b[:])
        nc.vector.tensor_copy(out=identb[:], in_=ident)
        waiting = []
        pks = [prep_tensor(AHEAD + 2)]
        for s in range(n_banks + LAG_DIRECT + 1):
            for lead, rows in ((1, (3,)), (2, (0, 1, 2))):
                if s + lead < n_banks and product_group(s + lead) is not None:
                    product(s + lead, rows)
            for q in spread_at.get(s, []):
                spread(q)
            if s + AHEAD + 3 < n_banks:
                pks.append(prep_tensor(s + AHEAD + 3))
            if s == PRODUCT_PREP:
                pks.append(prep_tensor(first_use[PRODUCT_GROUPS[-1]]))
            if s < n_banks:
                hidden(s)
            if s + 1 < n_banks and product_group(s + 1) is not None:
                spread(s + 2)
            if s < n_banks and product_group(s) is not None:
                spread(s + 2)
            if ends_unit(s - 1):
                regroup(unit_of[s - 1])
            for q in range(max(0, s - LAG_DIRECT), min(n_banks, s)):
                if direct_step(q) == s:
                    direct(q)
            if ends_unit(s - 2):
                quantise(unit_of[s - 2])
                for q in members(unit_of[s - 2]):
                    multiply(q)
            if 0 <= s - TAIL_PREP_AT < len(tail_shifts):
                shift_tail(*tail_shifts[s - TAIL_PREP_AT])
            if s - TAIL_PREP_AT == len(tail_shifts):
                nc.vector.tensor_copy(out=vt[:], in_=vtail[:, :, :])
            for b in range(LATE):
                if b in due:
                    size = sizes.get(b, N // 4)
                    mirror_blocks(b, size)
                    sizes[b] = size // 2
                    if size == ROWS:
                        due.remove(b)
                        for g in range(0, GROUPS, 4):
                            store_rows(b, g, g + 4)
            for q in range(max(0, s - LAG_DIRECT - 1), min(n_banks, s)):
                if direct_step(q) + 1 == s:
                    mirror_and_store(q)
                    if ends_unit(q):
                        mirror_unit(unit_of[q])
            for pk in waiting:
                prep_vector(pk)
            waiting = pks
            pks = []
            if 0 <= s - SPLIT_AT < PARTS:
                split(s - SPLIT_AT)
            for k, g in enumerate(reversed(PRODUCT_GROUPS)):
                if s == SPLIT_AT + PARTS + 2 * k - 1:
                    turn(g)
                if s == SPLIT_AT + PARTS + 2 * k:
                    nc.vector.tensor_copy(
                        out=drows[g][:].rearrange("p b j -> p (b j)"), in_=vrow.rearrange("p b j -> p (b j)")
                    )
        assert stored == [GROUPS for b in range(B)]
